import numpy as np
import ml_dtypes


def mxq(x, axis, fmt="e4m3"):
    dtype, down = {"e4m3": (ml_dtypes.float8_e4m3fn, 7), "e5m2": (ml_dtypes.float8_e5m2, 14)}[fmt]
    v = np.moveaxis(np.asarray(x, np.float32).astype(ml_dtypes.bfloat16).astype(np.float64), axis, -1)
    blocks = v.reshape(v.shape[:-1] + (-1, 32))
    amax = np.abs(blocks).max(-1, keepdims=True)
    byte = np.maximum(np.where(amax > 0, np.frexp(amax)[1] - 1 + 127, 0) - down, 1)
    scale = np.exp2(byte - 127.0)
    codes = (blocks / scale).astype(np.float32).astype(dtype).astype(np.float64)
    return np.moveaxis((codes * scale).reshape(v.shape), -1, axis)


WIDE = False


def mx_kscale(k):
    if not WIDE:
        return np.ones(k)
    levels = np.array([10, -10, 5, -5, 0])
    a = np.random.permutation(np.resize(levels, k // 512 * 4)).reshape(k // 512, 4)
    idx = np.arange(k)
    return np.exp2(a[idx // 512, idx % 128 // 32])


BF16 = ml_dtypes.bfloat16


def bf(x):
    return np.asarray(x, np.float32).astype(BF16)


def f64(x):
    return np.asarray(x).astype(np.float64)


B, S, A, O, H, L = 1024, 1024, 128, 1920, 1024, 384
G = L + A


def sigmoid(v):
    return 1.0 / (1.0 + np.exp(-v))


def setup_inputs():
    s = mx_kscale(G)
    return {"sample": bf(np.random.standard_normal((B, L)) * 1.1 * s[:L]),
            "prev_action": bf(np.random.standard_normal((B, A)) * s[L:]),
            "prev_state": bf(np.random.standard_normal((B, S))),
            "gru_Wih": bf(np.random.standard_normal((3 * H, G)) / np.sqrt(G) / s),
            "gru_Whh": bf(np.random.standard_normal((3 * H, H)) / np.sqrt(H)),
            "gru_bih": bf(np.random.standard_normal(3 * H) * 0.1),
            "gru_bhh": bf(np.random.standard_normal(3 * H) * 0.1)}


def reference(sample, prev_action, prev_state, gru_Wih, gru_Whh, gru_bih, gru_bhh):
    hp = f64(prev_state)
    xg = np.concatenate([f64(sample), f64(prev_action)], axis=-1)
    gi = (mxq(xg, 1, "e4m3") @ mxq(f64(gru_Wih), 1, "e4m3").T) + f64(gru_bih)
    gh = (mxq(hp, 1, "e4m3") @ mxq(f64(gru_Whh), 1, "e4m3").T) + f64(gru_bhh)
    gi_r, gi_z, gi_n = np.split(gi, 3, axis=-1)
    gh_r, gh_z, gh_n = np.split(gh, 3, axis=-1)
    r = sigmoid(gi_r + gh_r)
    z = sigmoid(gi_z + gh_z)
    n = np.tanh(gi_n + r * gh_n)
    belief = (1.0 - z) * n + z * hp
    return belief

@@ -1,0 +1,316 @@
+from contextlib import ExitStack
+
+import concourse.mybir as mybir
+from concourse.masks import make_identity
+
+F32 = mybir.dt.float32
+BF16 = mybir.dt.bfloat16
+U32 = mybir.dt.uint32
+U8 = mybir.dt.uint8
+FP8X4 = mybir.dt.float8_e4m3fn_x4
+ACT = mybir.ActivationFunctionType
+ALU = mybir.AluOpType
+
+P = 128
+BATCH = 1024
+HIDDEN = 1024
+LATENT = 384
+K_IN = 512
+GATES = 3
+PASSES = 3
+B_TILES = BATCH // P
+CHUNK = 512
+CHUNKS = BATCH // CHUNK
+CHUNK_TILES = CHUNK // P
+PAIR = 2 * P
+PAIRS = HIDDEN // PAIR
+ROUNDS = PAIRS * CHUNKS * 2
+BANK_WORDS = 512
+
+FLOPS = 2 * BATCH * GATES * HIDDEN * (K_IN + HIDDEN)
+
+
+def tile_rssm_pb_kernel(tc, sample, prev_action, prev_state, gru_Wih, gru_Whh, gru_bih, gru_bhh, out):
+    nc = tc.nc
+
+    sample_v = sample.rearrange("(p t) k -> p t k", t=B_TILES)
+    action_v = prev_action.rearrange("(p t) k -> p t k", t=B_TILES)
+    state_v = prev_state.rearrange("(p t) k -> p t k", t=B_TILES)
+    out_v = out.rearrange("(p t) h -> p t h", t=B_TILES)
+    wih_v = gru_Wih.rearrange("(g j q e) k -> g j q (e k)", g=GATES, j=PAIRS, e=2)
+    whh_v = gru_Whh.rearrange("(g j q e) k -> g j q (e k)", g=GATES, j=PAIRS, e=2)
+
+    with ExitStack() as ctx:
+        const = ctx.enter_context(tc.tile_pool(name="const", bufs=1))
+        x_keep = ctx.enter_context(tc.tile_pool(name="x_keep", bufs=CHUNKS))
+        w_rows = ctx.enter_context(tc.tile_pool(name="w_rows", bufs=2 * GATES))
+        w_grouped = ctx.enter_context(tc.tile_pool(name="w_grouped", bufs=2 * PASSES))
+        w_quant = ctx.enter_context(tc.tile_pool(name="w_quant", bufs=2 * GATES * PASSES))
+        gating = ctx.enter_context(tc.tile_pool(name="gating", bufs=3))
+        beliefs = ctx.enter_context(tc.tile_pool(name="beliefs", bufs=6))
+        results = ctx.enter_context(tc.tile_pool(name="results", bufs=2))
+        sums = ctx.enter_context(tc.psum_pool(name="sums", bufs=4))
+        flipped = ctx.enter_context(tc.psum_pool(name="flipped", bufs=4))
+        ctx.enter_context(tc.manual_schedule())
+
+
+        def drain(dst, bank_view, bank_index):
+            if bank_index % 2 == 0:
+                nc.scalar.copy(out=dst, in_=bank_view)
+            else:
+                nc.vector.tensor_copy(out=dst, in_=bank_view)
+
+        def flip_pass(in_words, hid_words, rows, g, grouped_words, bank_index):
+            bank = flipped.tile([P, 2, 2, P], F32, tag="bank")
+            for a in range(2):
+                for u in range(2):
+                    if g == 0:
+                        block = 2 * rows[a] + u
+                        words = in_words[:, block * P : (block + 1) * P]
+                    else:
+                        block = 4 * rows[a] + 2 * (g - 1) + u
+                        words = hid_words[:, block * P : (block + 1) * P]
+                    nc.tensor.transpose(bank[:, a, u, :], words, ident[:])
+            drain(
+                grouped_words.rearrange("p (a r u) -> p a r u", a=2, u=2),
+                bank[:].rearrange("p a u r -> p a r u"),
+                bank_index,
+            )
+
+
+        x_in_rows = []
+        x_hid_rows = []
+        x_grouped = []
+        x_codes = []
+        x_scales = []
+        for chunk in range(CHUNKS):
+            in_rows = x_keep.tile([P, CHUNK_TILES * K_IN], BF16)
+            hid_rows = x_keep.tile([P, CHUNK_TILES * HIDDEN], BF16)
+            grouped = x_keep.tile([P, PASSES * CHUNK * 4], BF16, align_bytes=64)
+            codes = x_keep.tile([P, PASSES * CHUNK], U32, align_bytes=64)
+            scales = x_keep.tile([P, PASSES * CHUNK], U8, align_bytes=64)
+            x_in_rows.append(in_rows)
+            x_hid_rows.append(hid_rows)
+            x_grouped.append(grouped)
+            x_codes.append(codes)
+            x_scales.append(scales)
+
+        def load_x(chunk):
+            tiles = slice(chunk * CHUNK_TILES, (chunk + 1) * CHUNK_TILES)
+            in_view = x_in_rows[chunk][:].rearrange("p (t k) -> p t k", t=CHUNK_TILES)
+            hid_view = x_hid_rows[chunk][:].rearrange("p (t k) -> p t k", t=CHUNK_TILES)
+            nc.sync.dma_start(out=in_view[:, :, 0:LATENT], in_=sample_v[:, tiles, :])
+            nc.sync.dma_start(out=in_view[:, :, LATENT:K_IN], in_=action_v[:, tiles, :])
+            nc.sync.dma_start(out=hid_view, in_=state_v[:, tiles, :])
+
+        def flip_x(chunk, half, first_bank):
+            grouped_words = x_grouped[chunk][:].bitcast(F32)
+            for g in range(PASSES):
+                start = (g * CHUNK + half * 2 * P) * 2
+                flip_pass(
+                    x_in_rows[chunk][:].bitcast(F32),
+                    x_hid_rows[chunk][:].bitcast(F32),
+                    [2 * half, 2 * half + 1],
+                    g,
+                    grouped_words[:, start : start + BANK_WORDS],
+                    first_bank + g,
+                )
+
+        def quantise_x(chunk, half):
+            for g in range(PASSES):
+                first = g * CHUNK + half * 2 * P
+                cols = slice(first, first + 2 * P)
+                nc.vector.quantize_mx(
+                    out=x_codes[chunk][:, cols].bitcast(FP8X4),
+                    scales=x_scales[chunk][:, cols],
+                    in_=x_grouped[chunk][:, 4 * first : 4 * (first + 2 * P)],
+                )
+
+
+        w_loaded = {}
+        w_flipped = {}
+        w_ready = {}
+
+        def load_w(pair, gate):
+            wih_rows = w_rows.tile([P, 2 * K_IN], BF16)
+            whh_rows = w_rows.tile([P, 2 * HIDDEN], BF16)
+            nc.sync.dma_start(out=wih_rows[:], in_=wih_v[gate, pair])
+            nc.sync.dma_start(out=whh_rows[:], in_=whh_v[gate, pair])
+            w_loaded[(pair, gate)] = (wih_rows, whh_rows)
+
+        def flip_w(pair, gate, first_bank):
+            wih_rows, whh_rows = w_loaded[(pair, gate)]
+            for g in range(PASSES):
+                w_pass = w_grouped.tile([P, 2 * P * 4], BF16, align_bytes=64)
+                flip_pass(
+                    wih_rows[:].bitcast(F32), whh_rows[:].bitcast(F32), [0, 1], g, w_pass[:].bitcast(F32), first_bank + g
+                )
+                w_flipped[(pair, gate, g)] = w_pass
+
+        def quantise_w(pair, gate):
+            for g in range(PASSES):
+                w_codes = w_quant.tile([P, 2 * P], U32, align_bytes=64)
+                w_scales = w_quant.tile([P, 2 * P], U8, align_bytes=64)
+                nc.vector.quantize_mx(
+                    out=w_codes[:].bitcast(FP8X4), scales=w_scales[:], in_=w_flipped[(pair, gate, g)][:]
+                )
+                w_ready[(pair, gate, g)] = (w_codes, w_scales)
+
+
+        def mx_group(pair, chunk, e, gate, passes):
+            acc = sums.tile([P, CHUNK], F32, tag="acc")
+            units = slice(e * P, (e + 1) * P)
+            for g in passes:
+                w_codes, w_scales = w_ready[(pair, gate, g)]
+                cols = slice(g * CHUNK, (g + 1) * CHUNK)
+                nc.tensor.matmul_mx(
+                    out=acc[:],
+                    lhsT=w_codes[:, units].bitcast(FP8X4),
+                    lhsT_scale=w_scales[:, units],
+                    rhs=x_codes[chunk][:, cols].bitcast(FP8X4),
+                    rhs_scale=x_scales[chunk][:, cols],
+                    start=(g == passes[0]),
+                    stop=(g == passes[-1]),
+                )
+            return acc
+
+        def bias_column(table, gate, pair, e):
+            column = (gate * PAIRS + pair) * 2 + e
+            return table[:, column : column + 1]
+
+        def products(pair, chunk, e):
+            acc_r = mx_group(pair, chunk, e, 0, [0, 1, 2])
+            r = gating.tile([P, CHUNK], F32)
+            nc.scalar.activation(out=r[:], in_=acc_r[:], func=ACT.Sigmoid, bias=bias_column(bias_both, 0, pair, e))
+            acc_z = mx_group(pair, chunk, e, 1, [0, 1, 2])
+            z = gating.tile([P, CHUNK], F32)
+            nc.scalar.activation(out=z[:], in_=acc_z[:], func=ACT.Sigmoid, bias=bias_column(bias_both, 1, pair, e))
+            state_t = x_grouped[chunk][:].rearrange("p (g b t) -> p g b t", g=PASSES, t=4)[
+                :, 1 + pair // 2, :, 2 * (pair % 2) + e
+            ]
+            kept = gating.tile([P, CHUNK], F32)
+            nc.gpsimd.tensor_tensor(out=kept[:], in0=z[:], in1=state_t, op=ALU.mult)
+            acc_hn = mx_group(pair, chunk, e, 2, [1, 2])
+            acc_in = mx_group(pair, chunk, e, 2, [0])
+            return {"where": (pair, chunk, e), "r": r, "z": z, "kept": kept, "acc_hn": acc_hn, "acc_in": acc_in}
+
+        def candidate_input(unit):
+            pair, chunk, e = unit["where"]
+            gated = gating.tile([P, CHUNK], F32)
+            nc.vector.scalar_tensor_tensor(
+                out=gated[:],
+                in0=unit["acc_hn"][:],
+                scalar=bias_column(bias_hid, 2, pair, e),
+                in1=unit["r"][:],
+                op0=ALU.add,
+                op1=ALU.mult,
+            )
+            pre_n = gating.tile([P, CHUNK], F32)
+            nc.vector.tensor_tensor(out=pre_n[:], in0=unit["acc_in"][:], in1=gated[:], op=ALU.add)
+            unit["pre_n"] = pre_n
+
+        def candidate(unit):
+            pair, chunk, e = unit["where"]
+            n = gating.tile([P, CHUNK], F32)
+            nc.scalar.activation(out=n[:], in_=unit["pre_n"][:], func=ACT.Tanh, bias=bias_column(bias_in, 2, pair, e))
+            unit["n"] = n
+
+        def blend(unit):
+            minus_new = gating.tile([P, CHUNK], F32)
+            nc.vector.scalar_tensor_tensor(
+                out=minus_new[:], in0=unit["z"][:], scalar=1.0, in1=unit["n"][:], op0=ALU.subtract, op1=ALU.mult
+            )
+            belief_t = beliefs.tile([P, CHUNK], F32)
+            nc.gpsimd.tensor_tensor(out=belief_t[:], in0=unit["kept"][:], in1=minus_new[:], op=ALU.subtract)
+            belief_tiles[unit["where"]] = belief_t
+
+        belief_tiles = {}
+
+        def return_chunk(pair, chunk, first_bank):
+            rows = results.tile([P, CHUNK_TILES, PAIR], F32)
+            for half in range(2):
+                bank = flipped.tile([P, 2, 2, P], F32, tag="bank")
+                for a in range(2):
+                    cols = slice((2 * half + a) * P, (2 * half + a + 1) * P)
+                    for e in range(2):
+                        nc.tensor.transpose(bank[:, a, e, :], belief_tiles[(pair, chunk, e)][:, cols], ident[:])
+                drain(
+                    rows[:, 2 * half : 2 * half + 2, :].rearrange("p a (q e) -> p a q e", e=2),
+                    bank[:].rearrange("p a e q -> p a q e"),
+                    first_bank + half,
+                )
+            tiles = slice(chunk * CHUNK_TILES, (chunk + 1) * CHUNK_TILES)
+            nc.sync.dma_start(out=out_v[:, tiles, pair * PAIR : (pair + 1) * PAIR], in_=rows[:])
+
+
+        bias_rows = const.tile([P, PAIR], BF16)
+        nc.vector.memset(bias_rows[:], 0.0)
+        n_rows = GATES * PAIRS
+        nc.scalar.dma_start(out=bias_rows[0:n_rows, :], in_=gru_bih.rearrange("(r w) -> r w", w=PAIR))
+        nc.scalar.dma_start(out=bias_rows[n_rows : 2 * n_rows, :], in_=gru_bhh.rearrange("(r w) -> r w", w=PAIR))
+        ident = const.tile([P, P], F32)
+        make_identity(nc, ident[:])
+
+        load_x(0)
+        for gate in range(GATES):
+            load_w(0, gate)
+        load_x(1)
+        for gate in range(GATES):
+            load_w(1, gate)
+
+        for half in range(2):
+            flip_x(0, half, 0)
+            quantise_x(0, half)
+
+        bias_bank = flipped.tile([P, BANK_WORDS], F32, tag="bank")
+        nc.tensor.transpose(bias_bank[:, 0:P], bias_rows[:].bitcast(F32), ident[:])
+        bias_all = const.tile([P, 4 * n_rows], F32)
+        nc.vector.tensor_copy(out=bias_all[:], in_=bias_bank[:].bitcast(BF16)[:, 0 : 4 * n_rows])
+        bias_in = bias_all[:, 0 : 2 * n_rows]
+        bias_hid = bias_all[:, 2 * n_rows : 4 * n_rows]
+        bias_both = const.tile([P, 2 * n_rows], F32)
+        nc.vector.tensor_tensor(out=bias_both[:], in0=bias_in, in1=bias_hid, op=ALU.add)
+
+        for gate in range(GATES):
+            flip_w(0, gate, 0)
+            quantise_w(0, gate)
+
+
+        unit = None
+        for rnd in range(ROUNDS):
+            pair, step = divmod(rnd, 2 * CHUNKS)
+            chunk, e = divmod(step, 2)
+            more_weights = pair + 1 < PAIRS and step < GATES
+
+            if unit is not None:
+                candidate_input(unit)
+
+            bank_index = 0
+            if more_weights:
+                flip_w(pair + 1, step, bank_index)
+                bank_index += PASSES
+            if rnd < 2:
+                flip_x(1, rnd, bank_index)
+                bank_index += PASSES
+            if pair > 0 and step % 2 == 0:
+                return_chunk(pair - 1, step // 2, bank_index)
+            if rnd == ROUNDS - 1:
+                return_chunk(pair, 0, bank_index)
+            if pair + 2 < PAIRS and step < GATES:
+                load_w(pair + 2, step)
+
+            if unit is not None:
+                candidate(unit)
+            if more_weights:
+                quantise_w(pair + 1, step)
+            if rnd < 2:
+                quantise_x(1, rnd)
+            if unit is not None:
+                blend(unit)
+
+            unit = products(pair, chunk, e)
+
+        candidate_input(unit)
+        candidate(unit)
+        blend(unit)
+        return_chunk(PAIRS - 1, CHUNKS - 1, 0)

@@ -25,6 +25,7 @@ CHUNK_TILES = CHUNK // P
 PAIR = 2 * P
 PAIRS = HIDDEN // PAIR
 ROUNDS = PAIRS * CHUNKS * 2
+RETURN_LAG = 3
 BANK_WORDS = 512
 
 FLOPS = 2 * BATCH * GATES * HIDDEN * (K_IN + HIDDEN)
@@ -48,19 +49,13 @@ def tile_rssm_pb_kernel(tc, sample, prev_action, prev_state, gru_Wih, gru_Whh, g
         w_quant = ctx.enter_context(tc.tile_pool(name="w_quant", bufs=2 * GATES * PASSES))
         gating = ctx.enter_context(tc.tile_pool(name="gating", bufs=3))
         beliefs = ctx.enter_context(tc.tile_pool(name="beliefs", bufs=6))
-        results = ctx.enter_context(tc.tile_pool(name="results", bufs=2))
+        results = ctx.enter_context(tc.tile_pool(name="results", bufs=3))
         sums = ctx.enter_context(tc.psum_pool(name="sums", bufs=4))
         flipped = ctx.enter_context(tc.psum_pool(name="flipped", bufs=4))
         ctx.enter_context(tc.manual_schedule())
 
 
-        def drain(dst, bank_view, bank_index):
-            if bank_index % 2 == 0:
-                nc.scalar.copy(out=dst, in_=bank_view)
-            else:
-                nc.vector.tensor_copy(out=dst, in_=bank_view)
-
-        def flip_pass(in_words, hid_words, rows, g, grouped_words, bank_index):
+        def flip_pass(in_words, hid_words, rows, g, grouped_words):
             bank = flipped.tile([P, 2, 2, P], F32, tag="bank")
             for a in range(2):
                 for u in range(2):
@@ -71,11 +66,12 @@ def tile_rssm_pb_kernel(tc, sample, prev_action, prev_state, gru_Wih, gru_Whh, g
                         block = 4 * rows[a] + 2 * (g - 1) + u
                         words = hid_words[:, block * P : (block + 1) * P]
                     nc.tensor.transpose(bank[:, a, u, :], words, ident[:])
-            drain(
-                grouped_words.rearrange("p (a r u) -> p a r u", a=2, u=2),
-                bank[:].rearrange("p a u r -> p a r u"),
-                bank_index,
-            )
+            dst = grouped_words.rearrange("p (a r u) -> p a r u", a=2, u=2)
+            src = bank[:].rearrange("p a u r -> p a r u")
+            if g == PASSES - 1:
+                nc.vector.tensor_copy(out=dst, in_=src)
+            else:
+                nc.scalar.copy(out=dst, in_=src)
 
 
         x_in_rows = []
@@ -103,7 +99,7 @@ def tile_rssm_pb_kernel(tc, sample, prev_action, prev_state, gru_Wih, gru_Whh, g
             nc.sync.dma_start(out=in_view[:, :, LATENT:K_IN], in_=action_v[:, tiles, :])
             nc.sync.dma_start(out=hid_view, in_=state_v[:, tiles, :])
 
-        def flip_x(chunk, half, first_bank):
+        def flip_x(chunk, half):
             grouped_words = x_grouped[chunk][:].bitcast(F32)
             for g in range(PASSES):
                 start = (g * CHUNK + half * 2 * P) * 2
@@ -113,7 +109,6 @@ def tile_rssm_pb_kernel(tc, sample, prev_action, prev_state, gru_Wih, gru_Whh, g
                     [2 * half, 2 * half + 1],
                     g,
                     grouped_words[:, start : start + BANK_WORDS],
-                    first_bank + g,
                 )
 
         def quantise_x(chunk, half):
@@ -138,13 +133,11 @@ def tile_rssm_pb_kernel(tc, sample, prev_action, prev_state, gru_Wih, gru_Whh, g
             nc.sync.dma_start(out=whh_rows[:], in_=whh_v[gate, pair])
             w_loaded[(pair, gate)] = (wih_rows, whh_rows)
 
-        def flip_w(pair, gate, first_bank):
+        def flip_w(pair, gate):
             wih_rows, whh_rows = w_loaded[(pair, gate)]
             for g in range(PASSES):
                 w_pass = w_grouped.tile([P, 2 * P * 4], BF16, align_bytes=64)
-                flip_pass(
-                    wih_rows[:].bitcast(F32), whh_rows[:].bitcast(F32), [0, 1], g, w_pass[:].bitcast(F32), first_bank + g
-                )
+                flip_pass(wih_rows[:].bitcast(F32), whh_rows[:].bitcast(F32), [0, 1], g, w_pass[:].bitcast(F32))
                 w_flipped[(pair, gate, g)] = w_pass
 
         def quantise_w(pair, gate):
@@ -221,26 +214,23 @@ def tile_rssm_pb_kernel(tc, sample, prev_action, prev_state, gru_Wih, gru_Whh, g
                 out=minus_new[:], in0=unit["z"][:], scalar=1.0, in1=unit["n"][:], op0=ALU.subtract, op1=ALU.mult
             )
             belief_t = beliefs.tile([P, CHUNK], F32)
-            nc.gpsimd.tensor_tensor(out=belief_t[:], in0=unit["kept"][:], in1=minus_new[:], op=ALU.subtract)
+            nc.vector.tensor_tensor(out=belief_t[:], in0=unit["kept"][:], in1=minus_new[:], op=ALU.subtract)
             belief_tiles[unit["where"]] = belief_t
 
         belief_tiles = {}
 
-        def return_chunk(pair, chunk, first_bank):
-            rows = results.tile([P, CHUNK_TILES, PAIR], F32)
-            for half in range(2):
-                bank = flipped.tile([P, 2, 2, P], F32, tag="bank")
-                for a in range(2):
-                    cols = slice((2 * half + a) * P, (2 * half + a + 1) * P)
-                    for e in range(2):
-                        nc.tensor.transpose(bank[:, a, e, :], belief_tiles[(pair, chunk, e)][:, cols], ident[:])
-                drain(
-                    rows[:, 2 * half : 2 * half + 2, :].rearrange("p a (q e) -> p a q e", e=2),
-                    bank[:].rearrange("p a e q -> p a q e"),
-                    first_bank + half,
-                )
-            tiles = slice(chunk * CHUNK_TILES, (chunk + 1) * CHUNK_TILES)
-            nc.sync.dma_start(out=out_v[:, tiles, pair * PAIR : (pair + 1) * PAIR], in_=rows[:])
+        def return_half(bank_number):
+            finished, half = divmod(bank_number, 2)
+            pair, chunk = divmod(finished, CHUNKS)
+            bank = flipped.tile([P, 2, 2, P], F32, tag="bank")
+            for a in range(2):
+                cols = slice((2 * half + a) * P, (2 * half + a + 1) * P)
+                for e in range(2):
+                    nc.tensor.transpose(bank[:, a, e, :], belief_tiles[(pair, chunk, e)][:, cols], ident[:])
+            rows = results.tile([P, 2, PAIR], F32)
+            nc.scalar.copy(out=rows[:].rearrange("p a (q e) -> p a q e", e=2), in_=bank[:].rearrange("p a e q -> p a q e"))
+            first_tile = chunk * CHUNK_TILES + 2 * half
+            nc.sync.dma_start(out=out_v[:, first_tile : first_tile + 2, pair * PAIR : (pair + 1) * PAIR], in_=rows[:])
 
 
         bias_rows = const.tile([P, PAIR], BF16)
@@ -259,7 +249,7 @@ def tile_rssm_pb_kernel(tc, sample, prev_action, prev_state, gru_Wih, gru_Whh, g
             load_w(1, gate)
 
         for half in range(2):
-            flip_x(0, half, 0)
+            flip_x(0, half)
             quantise_x(0, half)
 
         bias_bank = flipped.tile([P, BANK_WORDS], F32, tag="bank")
@@ -272,45 +262,31 @@ def tile_rssm_pb_kernel(tc, sample, prev_action, prev_state, gru_Wih, gru_Whh, g
         nc.vector.tensor_tensor(out=bias_both[:], in0=bias_in, in1=bias_hid, op=ALU.add)
 
         for gate in range(GATES):
-            flip_w(0, gate, 0)
+            flip_w(0, gate)
             quantise_w(0, gate)
 
 
-        unit = None
         for rnd in range(ROUNDS):
             pair, step = divmod(rnd, 2 * CHUNKS)
             chunk, e = divmod(step, 2)
             more_weights = pair + 1 < PAIRS and step < GATES
 
-            if unit is not None:
-                candidate_input(unit)
-
-            bank_index = 0
+            unit = products(pair, chunk, e)
+            candidate_input(unit)
             if more_weights:
-                flip_w(pair + 1, step, bank_index)
-                bank_index += PASSES
+                flip_w(pair + 1, step)
             if rnd < 2:
-                flip_x(1, rnd, bank_index)
-                bank_index += PASSES
-            if pair > 0 and step % 2 == 0:
-                return_chunk(pair - 1, step // 2, bank_index)
-            if rnd == ROUNDS - 1:
-                return_chunk(pair, 0, bank_index)
+                flip_x(1, rnd)
+            candidate(unit)
+            if rnd >= RETURN_LAG:
+                return_half(rnd - RETURN_LAG)
             if pair + 2 < PAIRS and step < GATES:
                 load_w(pair + 2, step)
-
-            if unit is not None:
-                candidate(unit)
             if more_weights:
                 quantise_w(pair + 1, step)
             if rnd < 2:
                 quantise_x(1, rnd)
-            if unit is not None:
-                blend(unit)
+            blend(unit)
 
-            unit = products(pair, chunk, e)
-
-        candidate_input(unit)
-        candidate(unit)
-        blend(unit)
-        return_chunk(PAIRS - 1, CHUNKS - 1, 0)
+        for bank_number in range(ROUNDS - RETURN_LAG, ROUNDS):
+            return_half(bank_number)

@@ -52,7 +52,6 @@ def tile_rssm_pb_kernel(tc, sample, prev_action, prev_state, gru_Wih, gru_Whh, g
         results = ctx.enter_context(tc.tile_pool(name="results", bufs=3))
         sums = ctx.enter_context(tc.psum_pool(name="sums", bufs=4))
         flipped = ctx.enter_context(tc.psum_pool(name="flipped", bufs=4))
-        ctx.enter_context(tc.manual_schedule())
 
 
         def flip_pass(in_words, hid_words, rows, g, grouped_words):

@@ -96,7 +96,10 @@ def tile_rssm_pb_kernel(tc, sample, prev_action, prev_state, gru_Wih, gru_Whh, g
             hid_view = x_hid_rows[chunk][:].rearrange("p (t k) -> p t k", t=CHUNK_TILES)
             nc.sync.dma_start(out=in_view[:, :, 0:LATENT], in_=sample_v[:, tiles, :])
             nc.sync.dma_start(out=in_view[:, :, LATENT:K_IN], in_=action_v[:, tiles, :])
-            nc.sync.dma_start(out=hid_view, in_=state_v[:, tiles, :])
+            for half in range(2):
+                pair_of_tiles = slice(2 * half, 2 * half + 2)
+                first_tile = chunk * CHUNK_TILES + 2 * half
+                nc.sync.dma_start(out=hid_view[:, pair_of_tiles, :], in_=state_v[:, first_tile : first_tile + 2, :])
 
         def flip_x(chunk, half):
             grouped_words = x_grouped[chunk][:].bitcast(F32)
@@ -170,10 +173,15 @@ def tile_rssm_pb_kernel(tc, sample, prev_action, prev_state, gru_Wih, gru_Whh, g
             column = (gate * PAIRS + pair) * 2 + e
             return table[:, column : column + 1]
 
-        def products(pair, chunk, e):
+        def reset_gate(unit):
+            pair, chunk, e = unit["where"]
             acc_r = mx_group(pair, chunk, e, 0, [0, 1, 2])
             r = gating.tile([P, CHUNK], F32)
             nc.scalar.activation(out=r[:], in_=acc_r[:], func=ACT.Sigmoid, bias=bias_column(bias_both, 0, pair, e))
+            unit["r"] = r
+
+        def update_gate(unit):
+            pair, chunk, e = unit["where"]
             acc_z = mx_group(pair, chunk, e, 1, [0, 1, 2])
             z = gating.tile([P, CHUNK], F32)
             nc.scalar.activation(out=z[:], in_=acc_z[:], func=ACT.Sigmoid, bias=bias_column(bias_both, 1, pair, e))
@@ -182,9 +190,13 @@ def tile_rssm_pb_kernel(tc, sample, prev_action, prev_state, gru_Wih, gru_Whh, g
             ]
             kept = gating.tile([P, CHUNK], F32)
             nc.gpsimd.tensor_tensor(out=kept[:], in0=z[:], in1=state_t, op=ALU.mult)
-            acc_hn = mx_group(pair, chunk, e, 2, [1, 2])
-            acc_in = mx_group(pair, chunk, e, 2, [0])
-            return {"where": (pair, chunk, e), "r": r, "z": z, "kept": kept, "acc_hn": acc_hn, "acc_in": acc_in}
+            unit["z"] = z
+            unit["kept"] = kept
+
+        def candidate_sums(unit):
+            pair, chunk, e = unit["where"]
+            unit["acc_hn"] = mx_group(pair, chunk, e, 2, [1, 2])
+            unit["acc_in"] = mx_group(pair, chunk, e, 2, [0])
 
         def candidate_input(unit):
             pair, chunk, e = unit["where"]
@@ -218,7 +230,7 @@ def tile_rssm_pb_kernel(tc, sample, prev_action, prev_state, gru_Wih, gru_Whh, g
 
         belief_tiles = {}
 
-        def return_half(bank_number):
+        def return_half(bank_number, copy_out):
             finished, half = divmod(bank_number, 2)
             pair, chunk = divmod(finished, CHUNKS)
             bank = flipped.tile([P, 2, 2, P], F32, tag="bank")
@@ -227,7 +239,7 @@ def tile_rssm_pb_kernel(tc, sample, prev_action, prev_state, gru_Wih, gru_Whh, g
                 for e in range(2):
                     nc.tensor.transpose(bank[:, a, e, :], belief_tiles[(pair, chunk, e)][:, cols], ident[:])
             rows = results.tile([P, 2, PAIR], F32)
-            nc.scalar.copy(out=rows[:].rearrange("p a (q e) -> p a q e", e=2), in_=bank[:].rearrange("p a e q -> p a q e"))
+            copy_out(out=rows[:].rearrange("p a (q e) -> p a q e", e=2), in_=bank[:].rearrange("p a e q -> p a q e"))
             first_tile = chunk * CHUNK_TILES + 2 * half
             nc.sync.dma_start(out=out_v[:, first_tile : first_tile + 2, pair * PAIR : (pair + 1) * PAIR], in_=rows[:])
 
@@ -260,32 +272,52 @@ def tile_rssm_pb_kernel(tc, sample, prev_action, prev_state, gru_Wih, gru_Whh, g
         bias_both = const.tile([P, 2 * n_rows], F32)
         nc.vector.tensor_tensor(out=bias_both[:], in0=bias_in, in1=bias_hid, op=ALU.add)
 
-        for gate in range(GATES):
-            flip_w(0, gate)
-            quantise_w(0, gate)
+        first_units = [{"where": (0, 0, 0)}, {"where": (0, 0, 1)}]
+        flip_w(0, 0)
+        quantise_w(0, 0)
+        flip_w(0, 1)
+        quantise_w(0, 1)
+        for unit in first_units:
+            reset_gate(unit)
+        flip_w(0, 2)
+        quantise_w(0, 2)
+        for unit in first_units:
+            update_gate(unit)
+        for unit in first_units:
+            candidate_sums(unit)
+            candidate_input(unit)
+        for half in range(2):
+            flip_x(1, half)
+            quantise_x(1, half)
+        flip_w(1, 0)
+        for unit in first_units:
+            candidate(unit)
+        load_w(2, 0)
+        quantise_w(1, 0)
+        for unit in first_units:
+            blend(unit)
 
 
-        for rnd in range(ROUNDS):
+        for rnd in range(2, ROUNDS):
             pair, step = divmod(rnd, 2 * CHUNKS)
             chunk, e = divmod(step, 2)
-            more_weights = pair + 1 < PAIRS and step < GATES
+            more_weights = pair + 1 < PAIRS and step > 0
 
-            unit = products(pair, chunk, e)
+            unit = {"where": (pair, chunk, e)}
+            reset_gate(unit)
+            update_gate(unit)
+            candidate_sums(unit)
             candidate_input(unit)
             if more_weights:
-                flip_w(pair + 1, step)
-            if rnd < 2:
-                flip_x(1, rnd)
+                flip_w(pair + 1, step - 1)
             candidate(unit)
             if rnd >= RETURN_LAG:
-                return_half(rnd - RETURN_LAG)
-            if pair + 2 < PAIRS and step < GATES:
-                load_w(pair + 2, step)
+                return_half(rnd - RETURN_LAG, nc.scalar.copy)
+            if pair + 2 < PAIRS and step > 0:
+                load_w(pair + 2, step - 1)
             if more_weights:
-                quantise_w(pair + 1, step)
-            if rnd < 2:
-                quantise_x(1, rnd)
+                quantise_w(pair + 1, step - 1)
             blend(unit)
 
         for bank_number in range(ROUNDS - RETURN_LAG, ROUNDS):
-            return_half(bank_number)
+            return_half(bank_number, nc.scalar.copy if bank_number % 2 == 0 else nc.vector.tensor_copy)

@@ -48,13 +48,14 @@ def tile_rssm_pb_kernel(tc, sample, prev_action, prev_state, gru_Wih, gru_Whh, g
         w_grouped = ctx.enter_context(tc.tile_pool(name="w_grouped", bufs=2 * PASSES))
         w_quant = ctx.enter_context(tc.tile_pool(name="w_quant", bufs=2 * GATES * PASSES))
         gating = ctx.enter_context(tc.tile_pool(name="gating", bufs=3))
-        beliefs = ctx.enter_context(tc.tile_pool(name="beliefs", bufs=6))
+        changes = ctx.enter_context(tc.tile_pool(name="changes", bufs=6))
         results = ctx.enter_context(tc.tile_pool(name="results", bufs=3))
         sums = ctx.enter_context(tc.psum_pool(name="sums", bufs=4))
         flipped = ctx.enter_context(tc.psum_pool(name="flipped", bufs=4))
+        ctx.enter_context(tc.manual_schedule())
 
 
-        def flip_pass(in_words, hid_words, rows, g, grouped_words):
+        def flip_pass(in_words, hid_words, rows, g, grouped_words, copy_out):
             bank = flipped.tile([P, 2, 2, P], F32, tag="bank")
             for a in range(2):
                 for u in range(2):
@@ -65,12 +66,10 @@ def tile_rssm_pb_kernel(tc, sample, prev_action, prev_state, gru_Wih, gru_Whh, g
                         block = 4 * rows[a] + 2 * (g - 1) + u
                         words = hid_words[:, block * P : (block + 1) * P]
                     nc.tensor.transpose(bank[:, a, u, :], words, ident[:])
-            dst = grouped_words.rearrange("p (a r u) -> p a r u", a=2, u=2)
-            src = bank[:].rearrange("p a u r -> p a r u")
-            if g == PASSES - 1:
-                nc.vector.tensor_copy(out=dst, in_=src)
-            else:
-                nc.scalar.copy(out=dst, in_=src)
+            copy_out(
+                out=grouped_words.rearrange("p (a r u) -> p a r u", a=2, u=2),
+                in_=bank[:].rearrange("p a u r -> p a r u"),
+            )
 
 
         x_in_rows = []
@@ -101,7 +100,7 @@ def tile_rssm_pb_kernel(tc, sample, prev_action, prev_state, gru_Wih, gru_Whh, g
                 first_tile = chunk * CHUNK_TILES + 2 * half
                 nc.sync.dma_start(out=hid_view[:, pair_of_tiles, :], in_=state_v[:, first_tile : first_tile + 2, :])
 
-        def flip_x(chunk, half):
+        def flip_x(chunk, half, copies):
             grouped_words = x_grouped[chunk][:].bitcast(F32)
             for g in range(PASSES):
                 start = (g * CHUNK + half * 2 * P) * 2
@@ -111,6 +110,7 @@ def tile_rssm_pb_kernel(tc, sample, prev_action, prev_state, gru_Wih, gru_Whh, g
                     [2 * half, 2 * half + 1],
                     g,
                     grouped_words[:, start : start + BANK_WORDS],
+                    copies[g],
                 )
 
         def quantise_x(chunk, half):
@@ -135,11 +135,13 @@ def tile_rssm_pb_kernel(tc, sample, prev_action, prev_state, gru_Wih, gru_Whh, g
             nc.sync.dma_start(out=whh_rows[:], in_=whh_v[gate, pair])
             w_loaded[(pair, gate)] = (wih_rows, whh_rows)
 
-        def flip_w(pair, gate):
+        def flip_w(pair, gate, copies):
             wih_rows, whh_rows = w_loaded[(pair, gate)]
             for g in range(PASSES):
                 w_pass = w_grouped.tile([P, 2 * P * 4], BF16, align_bytes=64)
-                flip_pass(wih_rows[:].bitcast(F32), whh_rows[:].bitcast(F32), [0, 1], g, w_pass[:].bitcast(F32))
+                flip_pass(
+                    wih_rows[:].bitcast(F32), whh_rows[:].bitcast(F32), [0, 1], g, w_pass[:].bitcast(F32), copies[g]
+                )
                 w_flipped[(pair, gate, g)] = w_pass
 
         def quantise_w(pair, gate):
@@ -183,22 +185,22 @@ def tile_rssm_pb_kernel(tc, sample, prev_action, prev_state, gru_Wih, gru_Whh, g
         def update_gate(unit):
             pair, chunk, e = unit["where"]
             acc_z = mx_group(pair, chunk, e, 1, [0, 1, 2])
-            z = gating.tile([P, CHUNK], F32)
-            nc.scalar.activation(out=z[:], in_=acc_z[:], func=ACT.Sigmoid, bias=bias_column(bias_both, 1, pair, e))
-            state_t = x_grouped[chunk][:].rearrange("p (g b t) -> p g b t", g=PASSES, t=4)[
-                :, 1 + pair // 2, :, 2 * (pair % 2) + e
-            ]
-            kept = gating.tile([P, CHUNK], F32)
-            nc.gpsimd.tensor_tensor(out=kept[:], in0=z[:], in1=state_t, op=ALU.mult)
-            unit["z"] = z
-            unit["kept"] = kept
+            one_minus_z = gating.tile([P, CHUNK], F32)
+            nc.scalar.activation(
+                out=one_minus_z[:],
+                in_=acc_z[:],
+                func=ACT.Sigmoid,
+                bias=bias_column(bias_both_negative, 1, pair, e),
+                scale=-1.0,
+            )
+            unit["one_minus_z"] = one_minus_z
 
         def candidate_sums(unit):
             pair, chunk, e = unit["where"]
             unit["acc_hn"] = mx_group(pair, chunk, e, 2, [1, 2])
             unit["acc_in"] = mx_group(pair, chunk, e, 2, [0])
 
-        def candidate_input(unit):
+        def gate_hidden(unit):
             pair, chunk, e = unit["where"]
             gated = gating.tile([P, CHUNK], F32)
             nc.vector.scalar_tensor_tensor(
@@ -209,8 +211,11 @@ def tile_rssm_pb_kernel(tc, sample, prev_action, prev_state, gru_Wih, gru_Whh, g
                 op0=ALU.add,
                 op1=ALU.mult,
             )
+            unit["gated"] = gated
+
+        def candidate_input(unit):
             pre_n = gating.tile([P, CHUNK], F32)
-            nc.vector.tensor_tensor(out=pre_n[:], in0=unit["acc_in"][:], in1=gated[:], op=ALU.add)
+            nc.vector.tensor_tensor(out=pre_n[:], in0=unit["acc_in"][:], in1=unit["gated"][:], op=ALU.add)
             unit["pre_n"] = pre_n
 
         def candidate(unit):
@@ -219,29 +224,47 @@ def tile_rssm_pb_kernel(tc, sample, prev_action, prev_state, gru_Wih, gru_Whh, g
             nc.scalar.activation(out=n[:], in_=unit["pre_n"][:], func=ACT.Tanh, bias=bias_column(bias_in, 2, pair, e))
             unit["n"] = n
 
-        def blend(unit):
-            minus_new = gating.tile([P, CHUNK], F32)
-            nc.vector.scalar_tensor_tensor(
-                out=minus_new[:], in0=unit["z"][:], scalar=1.0, in1=unit["n"][:], op0=ALU.subtract, op1=ALU.mult
-            )
-            belief_t = beliefs.tile([P, CHUNK], F32)
-            nc.vector.tensor_tensor(out=belief_t[:], in0=unit["kept"][:], in1=minus_new[:], op=ALU.subtract)
-            belief_tiles[unit["where"]] = belief_t
 
-        belief_tiles = {}
+        def difference(unit):
+            pair, chunk, e = unit["where"]
+            state_t = x_grouped[chunk][:].rearrange("p (g b t) -> p g b t", g=PASSES, t=4)[
+                :, 1 + pair // 2, :, 2 * (pair % 2) + e
+            ]
+            away = gating.tile([P, CHUNK], F32)
+            nc.vector.tensor_tensor(out=away[:], in0=unit["n"][:], in1=state_t, op=ALU.subtract)
+            unit["away"] = away
 
-        def return_half(bank_number, copy_out):
+        def change(unit):
+            change_t = changes.tile([P, CHUNK], F32)
+            nc.vector.tensor_tensor(out=change_t[:], in0=unit["one_minus_z"][:], in1=unit["away"][:], op=ALU.mult)
+            change_tiles[unit["where"]] = change_t
+
+        change_tiles = {}
+
+        def flip_results(bank_number):
             finished, half = divmod(bank_number, 2)
             pair, chunk = divmod(finished, CHUNKS)
             bank = flipped.tile([P, 2, 2, P], F32, tag="bank")
             for a in range(2):
                 cols = slice((2 * half + a) * P, (2 * half + a + 1) * P)
                 for e in range(2):
-                    nc.tensor.transpose(bank[:, a, e, :], belief_tiles[(pair, chunk, e)][:, cols], ident[:])
+                    nc.tensor.transpose(bank[:, a, e, :], change_tiles[(pair, chunk, e)][:, cols], ident[:])
+            return bank
+
+        def add_state_and_store(bank_number, bank):
+            finished, half = divmod(bank_number, 2)
+            pair, chunk = divmod(finished, CHUNKS)
+            units = slice(pair * PAIR, (pair + 1) * PAIR)
+            state_rows = x_hid_rows[chunk][:].rearrange("p (t h) -> p t h", t=CHUNK_TILES)[:, 2 * half : 2 * half + 2, units]
             rows = results.tile([P, 2, PAIR], F32)
-            copy_out(out=rows[:].rearrange("p a (q e) -> p a q e", e=2), in_=bank[:].rearrange("p a e q -> p a q e"))
+            nc.vector.tensor_tensor(
+                out=rows[:].rearrange("p a (q e) -> p a q e", e=2),
+                in0=bank[:].rearrange("p a e q -> p a q e"),
+                in1=state_rows.rearrange("p a (q e) -> p a q e", e=2),
+                op=ALU.add,
+            )
             first_tile = chunk * CHUNK_TILES + 2 * half
-            nc.sync.dma_start(out=out_v[:, first_tile : first_tile + 2, pair * PAIR : (pair + 1) * PAIR], in_=rows[:])
+            nc.sync.dma_start(out=out_v[:, first_tile : first_tile + 2, units], in_=rows[:])
 
 
         bias_rows = const.tile([P, PAIR], BF16)
@@ -252,6 +275,9 @@ def tile_rssm_pb_kernel(tc, sample, prev_action, prev_state, gru_Wih, gru_Whh, g
         ident = const.tile([P, P], F32)
         make_identity(nc, ident[:])
 
+        shared = [nc.scalar.copy, nc.scalar.copy, nc.vector.tensor_copy]
+        scalar_only = [nc.scalar.copy, nc.scalar.copy, nc.scalar.copy]
+
         load_x(0)
         for gate in range(GATES):
             load_w(0, gate)
@@ -260,7 +286,7 @@ def tile_rssm_pb_kernel(tc, sample, prev_action, prev_state, gru_Wih, gru_Whh, g
             load_w(1, gate)
 
         for half in range(2):
-            flip_x(0, half)
+            flip_x(0, half, shared)
             quantise_x(0, half)
 
         bias_bank = flipped.tile([P, BANK_WORDS], F32, tag="bank")
@@ -271,31 +297,37 @@ def tile_rssm_pb_kernel(tc, sample, prev_action, prev_state, gru_Wih, gru_Whh, g
         bias_hid = bias_all[:, 2 * n_rows : 4 * n_rows]
         bias_both = const.tile([P, 2 * n_rows], F32)
         nc.vector.tensor_tensor(out=bias_both[:], in0=bias_in, in1=bias_hid, op=ALU.add)
+        bias_both_negative = const.tile([P, 2 * n_rows], F32)
+        nc.vector.tensor_scalar_mul(out=bias_both_negative[:], in0=bias_both[:], scalar1=-1.0)
 
         first_units = [{"where": (0, 0, 0)}, {"where": (0, 0, 1)}]
-        flip_w(0, 0)
+        flip_w(0, 0, shared)
         quantise_w(0, 0)
-        flip_w(0, 1)
+        flip_w(0, 1, shared)
         quantise_w(0, 1)
         for unit in first_units:
             reset_gate(unit)
-        flip_w(0, 2)
+        flip_w(0, 2, shared)
         quantise_w(0, 2)
         for unit in first_units:
             update_gate(unit)
         for unit in first_units:
             candidate_sums(unit)
+            gate_hidden(unit)
+        for unit in first_units:
             candidate_input(unit)
         for half in range(2):
-            flip_x(1, half)
+            flip_x(1, half, scalar_only)
             quantise_x(1, half)
-        flip_w(1, 0)
+        flip_w(1, 0, scalar_only)
         for unit in first_units:
             candidate(unit)
         load_w(2, 0)
         quantise_w(1, 0)
         for unit in first_units:
-            blend(unit)
+            difference(unit)
+        change(first_units[0])
+        previous = first_units[1]
 
 
         for rnd in range(2, ROUNDS):
@@ -307,17 +339,24 @@ def tile_rssm_pb_kernel(tc, sample, prev_action, prev_state, gru_Wih, gru_Whh, g
             reset_gate(unit)
             update_gate(unit)
             candidate_sums(unit)
+            gate_hidden(unit)
+            change(previous)
             candidate_input(unit)
             if more_weights:
-                flip_w(pair + 1, step - 1)
+                flip_w(pair + 1, step - 1, scalar_only)
             candidate(unit)
             if rnd >= RETURN_LAG:
-                return_half(rnd - RETURN_LAG, nc.scalar.copy)
+                bank = flip_results(rnd - RETURN_LAG)
             if pair + 2 < PAIRS and step > 0:
                 load_w(pair + 2, step - 1)
             if more_weights:
                 quantise_w(pair + 1, step - 1)
-            blend(unit)
+            difference(unit)
+            if rnd >= RETURN_LAG:
+                add_state_and_store(rnd - RETURN_LAG, bank)
+            previous = unit
 
+        change(previous)
         for bank_number in range(ROUNDS - RETURN_LAG, ROUNDS):
-            return_half(bank_number, nc.scalar.copy if bank_number % 2 == 0 else nc.vector.tensor_copy)
+            bank = flip_results(bank_number)
+            add_state_and_store(bank_number, bank)

@@ -317,15 +317,14 @@ def tile_rssm_pb_kernel(tc, sample, prev_action, prev_state, gru_Wih, gru_Whh, g
         for unit in first_units:
             candidate_input(unit)
         for half in range(2):
-            flip_x(1, half, scalar_only)
+            flip_x(1, half, shared)
             quantise_x(1, half)
-        flip_w(1, 0, scalar_only)
+        flip_w(1, 0, shared)
         for unit in first_units:
             candidate(unit)
         load_w(2, 0)
+        difference(first_units[0])
         quantise_w(1, 0)
-        for unit in first_units:
-            difference(unit)
         change(first_units[0])
         previous = first_units[1]
 
@@ -340,8 +339,9 @@ def tile_rssm_pb_kernel(tc, sample, prev_action, prev_state, gru_Wih, gru_Whh, g
             update_gate(unit)
             candidate_sums(unit)
             gate_hidden(unit)
-            change(previous)
+            difference(previous)
             candidate_input(unit)
+            change(previous)
             if more_weights:
                 flip_w(pair + 1, step - 1, scalar_only)
             candidate(unit)
@@ -351,12 +351,14 @@ def tile_rssm_pb_kernel(tc, sample, prev_action, prev_state, gru_Wih, gru_Whh, g
                 load_w(pair + 2, step - 1)
             if more_weights:
                 quantise_w(pair + 1, step - 1)
-            difference(unit)
             if rnd >= RETURN_LAG:
                 add_state_and_store(rnd - RETURN_LAG, bank)
             previous = unit
 
+        difference(previous)
+        bank = flip_results(ROUNDS - RETURN_LAG)
+        add_state_and_store(ROUNDS - RETURN_LAG, bank)
         change(previous)
-        for bank_number in range(ROUNDS - RETURN_LAG, ROUNDS):
+        for bank_number in range(ROUNDS - RETURN_LAG + 1, ROUNDS):
             bank = flip_results(bank_number)
             add_state_and_store(bank_number, bank)

@@ -225,13 +225,13 @@ def tile_rssm_pb_kernel(tc, sample, prev_action, prev_state, gru_Wih, gru_Whh, g
             unit["n"] = n
 
 
-        def difference(unit):
+        def difference(unit, engine):
             pair, chunk, e = unit["where"]
             state_t = x_grouped[chunk][:].rearrange("p (g b t) -> p g b t", g=PASSES, t=4)[
                 :, 1 + pair // 2, :, 2 * (pair % 2) + e
             ]
             away = gating.tile([P, CHUNK], F32)
-            nc.vector.tensor_tensor(out=away[:], in0=unit["n"][:], in1=state_t, op=ALU.subtract)
+            engine.tensor_tensor(out=away[:], in0=unit["n"][:], in1=state_t, op=ALU.subtract)
             unit["away"] = away
 
         def change(unit):
@@ -322,8 +322,8 @@ def tile_rssm_pb_kernel(tc, sample, prev_action, prev_state, gru_Wih, gru_Whh, g
         flip_w(1, 0, shared)
         for unit in first_units:
             candidate(unit)
+            difference(unit, nc.gpsimd)
         load_w(2, 0)
-        difference(first_units[0])
         quantise_w(1, 0)
         change(first_units[0])
         previous = first_units[1]
@@ -339,12 +339,13 @@ def tile_rssm_pb_kernel(tc, sample, prev_action, prev_state, gru_Wih, gru_Whh, g
             update_gate(unit)
             candidate_sums(unit)
             gate_hidden(unit)
-            difference(previous)
             candidate_input(unit)
             change(previous)
             if more_weights:
                 flip_w(pair + 1, step - 1, scalar_only)
             candidate(unit)
+            if rnd < ROUNDS - 1:
+                difference(unit, nc.gpsimd)
             if rnd >= RETURN_LAG:
                 bank = flip_results(rnd - RETURN_LAG)
             if pair + 2 < PAIRS and step > 0:
@@ -355,7 +356,7 @@ def tile_rssm_pb_kernel(tc, sample, prev_action, prev_state, gru_Wih, gru_Whh, g
                 add_state_and_store(rnd - RETURN_LAG, bank)
             previous = unit
 
-        difference(previous)
+        difference(previous, nc.vector)
         bank = flip_results(ROUNDS - RETURN_LAG)
         add_state_and_store(ROUNDS - RETURN_LAG, bank)
         change(previous)

@@ -51,12 +51,20 @@ def tile_rssm_pb_kernel(tc, sample, prev_action, prev_state, gru_Wih, gru_Whh, g
         changes = ctx.enter_context(tc.tile_pool(name="changes", bufs=6))
         results = ctx.enter_context(tc.tile_pool(name="results", bufs=3))
         sums = ctx.enter_context(tc.psum_pool(name="sums", bufs=4))
-        flipped = ctx.enter_context(tc.psum_pool(name="flipped", bufs=4))
+        flipped = ctx.enter_context(tc.psum_pool(name="flipped", bufs=1))
+        apart = ctx.enter_context(tc.tile_pool(name="apart", bufs=1))
         ctx.enter_context(tc.manual_schedule())
 
 
-        def flip_pass(in_words, hid_words, rows, g, grouped_words, copy_out):
-            bank = flipped.tile([P, 2, 2, P], F32, tag="bank")
+        banks_taken = [0]
+
+        def next_bank():
+            number = banks_taken[0] % 4
+            banks_taken[0] += 1
+            bank = flipped.tile([P, 2, 2, P], F32, tag="bank" + str(number))
+            return bank
+
+        def flip_pass(in_words, hid_words, rows, g, grouped_words, copy_out, bank):
             for a in range(2):
                 for u in range(2):
                     if g == 0:
@@ -111,6 +119,7 @@ def tile_rssm_pb_kernel(tc, sample, prev_action, prev_state, gru_Wih, gru_Whh, g
                     g,
                     grouped_words[:, start : start + BANK_WORDS],
                     copies[g],
+                    next_bank(),
                 )
 
         def quantise_x(chunk, half):
@@ -135,12 +144,18 @@ def tile_rssm_pb_kernel(tc, sample, prev_action, prev_state, gru_Wih, gru_Whh, g
             nc.sync.dma_start(out=whh_rows[:], in_=whh_v[gate, pair])
             w_loaded[(pair, gate)] = (wih_rows, whh_rows)
 
-        def flip_w(pair, gate, copies):
+        def flip_w(pair, gate, copies, banks):
             wih_rows, whh_rows = w_loaded[(pair, gate)]
             for g in range(PASSES):
                 w_pass = w_grouped.tile([P, 2 * P * 4], BF16, align_bytes=64)
                 flip_pass(
-                    wih_rows[:].bitcast(F32), whh_rows[:].bitcast(F32), [0, 1], g, w_pass[:].bitcast(F32), copies[g]
+                    wih_rows[:].bitcast(F32),
+                    whh_rows[:].bitcast(F32),
+                    [0, 1],
+                    g,
+                    w_pass[:].bitcast(F32),
+                    copies[g],
+                    banks(g),
                 )
                 w_flipped[(pair, gate, g)] = w_pass
 
@@ -230,7 +245,7 @@ def tile_rssm_pb_kernel(tc, sample, prev_action, prev_state, gru_Wih, gru_Whh, g
             state_t = x_grouped[chunk][:].rearrange("p (g b t) -> p g b t", g=PASSES, t=4)[
                 :, 1 + pair // 2, :, 2 * (pair % 2) + e
             ]
-            away = gating.tile([P, CHUNK], F32)
+            away = apart.tile([P, CHUNK], F32)
             engine.tensor_tensor(out=away[:], in0=unit["n"][:], in1=state_t, op=ALU.subtract)
             unit["away"] = away
 
@@ -241,10 +256,10 @@ def tile_rssm_pb_kernel(tc, sample, prev_action, prev_state, gru_Wih, gru_Whh, g
 
         change_tiles = {}
 
-        def flip_results(bank_number):
+        def flip_results(bank_number, bank_tag=3):
             finished, half = divmod(bank_number, 2)
             pair, chunk = divmod(finished, CHUNKS)
-            bank = flipped.tile([P, 2, 2, P], F32, tag="bank")
+            bank = flipped.tile([P, 2, 2, P], F32, tag="bank" + str(bank_tag))
             for a in range(2):
                 cols = slice((2 * half + a) * P, (2 * half + a + 1) * P)
                 for e in range(2):
@@ -289,10 +304,11 @@ def tile_rssm_pb_kernel(tc, sample, prev_action, prev_state, gru_Wih, gru_Whh, g
             flip_x(0, half, shared)
             quantise_x(0, half)
 
-        bias_bank = flipped.tile([P, BANK_WORDS], F32, tag="bank")
+        bias_tile = next_bank()
+        bias_bank = bias_tile[:].rearrange("p a u r -> p (a u r)")
         nc.tensor.transpose(bias_bank[:, 0:P], bias_rows[:].bitcast(F32), ident[:])
         bias_all = const.tile([P, 4 * n_rows], F32)
-        nc.vector.tensor_copy(out=bias_all[:], in_=bias_bank[:].bitcast(BF16)[:, 0 : 4 * n_rows])
+        nc.vector.tensor_copy(out=bias_all[:], in_=bias_bank.bitcast(BF16)[:, 0 : 4 * n_rows])
         bias_in = bias_all[:, 0 : 2 * n_rows]
         bias_hid = bias_all[:, 2 * n_rows : 4 * n_rows]
         bias_both = const.tile([P, 2 * n_rows], F32)
@@ -301,13 +317,13 @@ def tile_rssm_pb_kernel(tc, sample, prev_action, prev_state, gru_Wih, gru_Whh, g
         nc.vector.tensor_scalar_mul(out=bias_both_negative[:], in0=bias_both[:], scalar1=-1.0)
 
         first_units = [{"where": (0, 0, 0)}, {"where": (0, 0, 1)}]
-        flip_w(0, 0, shared)
+        flip_w(0, 0, shared, lambda g: next_bank())
         quantise_w(0, 0)
-        flip_w(0, 1, shared)
+        flip_w(0, 1, shared, lambda g: next_bank())
         quantise_w(0, 1)
         for unit in first_units:
             reset_gate(unit)
-        flip_w(0, 2, shared)
+        flip_w(0, 2, shared, lambda g: next_bank())
         quantise_w(0, 2)
         for unit in first_units:
             update_gate(unit)
@@ -319,16 +335,21 @@ def tile_rssm_pb_kernel(tc, sample, prev_action, prev_state, gru_Wih, gru_Whh, g
         for half in range(2):
             flip_x(1, half, shared)
             quantise_x(1, half)
-        flip_w(1, 0, shared)
+        flip_w(1, 0, shared, lambda g: next_bank())
         for unit in first_units:
             candidate(unit)
-            difference(unit, nc.gpsimd)
+        difference(first_units[0], nc.gpsimd)
         load_w(2, 0)
         quantise_w(1, 0)
         change(first_units[0])
         previous = first_units[1]
 
+        def weight_bank(g):
+            bank = flipped.tile([P, 2, 2, P], F32, tag="bank" + str(g))
+            return bank
 
+
+        waiting = []
         for rnd in range(2, ROUNDS):
             pair, step = divmod(rnd, 2 * CHUNKS)
             chunk, e = divmod(step, 2)
@@ -338,28 +359,29 @@ def tile_rssm_pb_kernel(tc, sample, prev_action, prev_state, gru_Wih, gru_Whh, g
             reset_gate(unit)
             update_gate(unit)
             candidate_sums(unit)
+            difference(previous, nc.gpsimd)
             gate_hidden(unit)
+            for bank_number, bank in waiting:
+                add_state_and_store(bank_number, bank)
+            waiting = []
             candidate_input(unit)
-            change(previous)
             if more_weights:
-                flip_w(pair + 1, step - 1, scalar_only)
+                flip_w(pair + 1, step - 1, scalar_only, weight_bank)
             candidate(unit)
-            if rnd < ROUNDS - 1:
-                difference(unit, nc.gpsimd)
             if rnd >= RETURN_LAG:
-                bank = flip_results(rnd - RETURN_LAG)
+                waiting.append((rnd - RETURN_LAG, flip_results(rnd - RETURN_LAG)))
             if pair + 2 < PAIRS and step > 0:
                 load_w(pair + 2, step - 1)
             if more_weights:
                 quantise_w(pair + 1, step - 1)
-            if rnd >= RETURN_LAG:
-                add_state_and_store(rnd - RETURN_LAG, bank)
+            change(previous)
             previous = unit
 
+        waiting.append((ROUNDS - RETURN_LAG, flip_results(ROUNDS - RETURN_LAG, 2)))
         difference(previous, nc.vector)
-        bank = flip_results(ROUNDS - RETURN_LAG)
-        add_state_and_store(ROUNDS - RETURN_LAG, bank)
+        for bank_number, bank in waiting:
+            add_state_and_store(bank_number, bank)
         change(previous)
         for bank_number in range(ROUNDS - RETURN_LAG + 1, ROUNDS):
-            bank = flip_results(bank_number)
+            bank = flip_results(bank_number, bank_number % 2)
             add_state_and_store(bank_number, bank)

@@ -28,6 +28,9 @@ ROUNDS = PAIRS * CHUNKS * 2
 RETURN_LAG = 3
 BANK_WORDS = 512
 
+EVERY = slice(0, CHUNK)
+HALVES = [slice(0, PAIR), slice(PAIR, 2 * PAIR)]
+
 FLOPS = 2 * BATCH * GATES * HIDDEN * (K_IN + HIDDEN)
 
 
@@ -49,7 +52,7 @@ def tile_rssm_pb_kernel(tc, sample, prev_action, prev_state, gru_Wih, gru_Whh, g
         w_quant = ctx.enter_context(tc.tile_pool(name="w_quant", bufs=2 * GATES * PASSES))
         gating = ctx.enter_context(tc.tile_pool(name="gating", bufs=3))
         changes = ctx.enter_context(tc.tile_pool(name="changes", bufs=6))
-        results = ctx.enter_context(tc.tile_pool(name="results", bufs=3))
+        results = ctx.enter_context(tc.tile_pool(name="results", bufs=5))
         sums = ctx.enter_context(tc.psum_pool(name="sums", bufs=4))
         flipped = ctx.enter_context(tc.psum_pool(name="flipped", bufs=1))
         apart = ctx.enter_context(tc.tile_pool(name="apart", bufs=1))
@@ -108,29 +111,26 @@ def tile_rssm_pb_kernel(tc, sample, prev_action, prev_state, gru_Wih, gru_Whh, g
                 first_tile = chunk * CHUNK_TILES + 2 * half
                 nc.sync.dma_start(out=hid_view[:, pair_of_tiles, :], in_=state_v[:, first_tile : first_tile + 2, :])
 
-        def flip_x(chunk, half, copies):
-            grouped_words = x_grouped[chunk][:].bitcast(F32)
-            for g in range(PASSES):
-                start = (g * CHUNK + half * 2 * P) * 2
-                flip_pass(
-                    x_in_rows[chunk][:].bitcast(F32),
-                    x_hid_rows[chunk][:].bitcast(F32),
-                    [2 * half, 2 * half + 1],
-                    g,
-                    grouped_words[:, start : start + BANK_WORDS],
-                    copies[g],
-                    next_bank(),
-                )
+        def flip_x(chunk, half, g, copy_out):
+            start = (g * CHUNK + half * 2 * P) * 2
+            flip_pass(
+                x_in_rows[chunk][:].bitcast(F32),
+                x_hid_rows[chunk][:].bitcast(F32),
+                [2 * half, 2 * half + 1],
+                g,
+                x_grouped[chunk][:].bitcast(F32)[:, start : start + BANK_WORDS],
+                copy_out,
+                next_bank(),
+            )
 
-        def quantise_x(chunk, half):
-            for g in range(PASSES):
-                first = g * CHUNK + half * 2 * P
-                cols = slice(first, first + 2 * P)
-                nc.vector.quantize_mx(
-                    out=x_codes[chunk][:, cols].bitcast(FP8X4),
-                    scales=x_scales[chunk][:, cols],
-                    in_=x_grouped[chunk][:, 4 * first : 4 * (first + 2 * P)],
-                )
+        def quantise_x(chunk, half, g):
+            first = g * CHUNK + half * 2 * P
+            cols = slice(first, first + 2 * P)
+            nc.vector.quantize_mx(
+                out=x_codes[chunk][:, cols].bitcast(FP8X4),
+                scales=x_scales[chunk][:, cols],
+                in_=x_grouped[chunk][:, 4 * first : 4 * (first + 2 * P)],
+            )
 
 
         w_loaded = {}
@@ -144,29 +144,21 @@ def tile_rssm_pb_kernel(tc, sample, prev_action, prev_state, gru_Wih, gru_Whh, g
             nc.sync.dma_start(out=whh_rows[:], in_=whh_v[gate, pair])
             w_loaded[(pair, gate)] = (wih_rows, whh_rows)
 
-        def flip_w(pair, gate, copies, banks):
+        def flip_w(pair, gate, g, copy_out, bank):
             wih_rows, whh_rows = w_loaded[(pair, gate)]
-            for g in range(PASSES):
-                w_pass = w_grouped.tile([P, 2 * P * 4], BF16, align_bytes=64)
-                flip_pass(
-                    wih_rows[:].bitcast(F32),
-                    whh_rows[:].bitcast(F32),
-                    [0, 1],
-                    g,
-                    w_pass[:].bitcast(F32),
-                    copies[g],
-                    banks(g),
-                )
-                w_flipped[(pair, gate, g)] = w_pass
+            w_pass = w_grouped.tile([P, 2 * P * 4], BF16, align_bytes=64)
+            flip_pass(
+                wih_rows[:].bitcast(F32), whh_rows[:].bitcast(F32), [0, 1], g, w_pass[:].bitcast(F32), copy_out, bank
+            )
+            w_flipped[(pair, gate, g)] = w_pass
 
-        def quantise_w(pair, gate):
-            for g in range(PASSES):
-                w_codes = w_quant.tile([P, 2 * P], U32, align_bytes=64)
-                w_scales = w_quant.tile([P, 2 * P], U8, align_bytes=64)
-                nc.vector.quantize_mx(
-                    out=w_codes[:].bitcast(FP8X4), scales=w_scales[:], in_=w_flipped[(pair, gate, g)][:]
-                )
-                w_ready[(pair, gate, g)] = (w_codes, w_scales)
+        def quantise_w(pair, gate, g):
+            w_codes = w_quant.tile([P, 2 * P], U32, align_bytes=64)
+            w_scales = w_quant.tile([P, 2 * P], U8, align_bytes=64)
+            nc.vector.quantize_mx(
+                out=w_codes[:].bitcast(FP8X4), scales=w_scales[:], in_=w_flipped[(pair, gate, g)][:]
+            )
+            w_ready[(pair, gate, g)] = (w_codes, w_scales)
 
 
         def mx_group(pair, chunk, e, gate, passes):
@@ -215,44 +207,61 @@ def tile_rssm_pb_kernel(tc, sample, prev_action, prev_state, gru_Wih, gru_Whh, g
             unit["acc_hn"] = mx_group(pair, chunk, e, 2, [1, 2])
             unit["acc_in"] = mx_group(pair, chunk, e, 2, [0])
 
-        def gate_hidden(unit):
+        def gate_hidden(unit, cols=EVERY):
             pair, chunk, e = unit["where"]
-            gated = gating.tile([P, CHUNK], F32)
+            if "gated" not in unit:
+                gated = gating.tile([P, CHUNK], F32)
+                unit["gated"] = gated
             nc.vector.scalar_tensor_tensor(
-                out=gated[:],
-                in0=unit["acc_hn"][:],
+                out=unit["gated"][:, cols],
+                in0=unit["acc_hn"][:, cols],
                 scalar=bias_column(bias_hid, 2, pair, e),
-                in1=unit["r"][:],
+                in1=unit["r"][:, cols],
                 op0=ALU.add,
                 op1=ALU.mult,
             )
-            unit["gated"] = gated
 
-        def candidate_input(unit):
-            pre_n = gating.tile([P, CHUNK], F32)
-            nc.vector.tensor_tensor(out=pre_n[:], in0=unit["acc_in"][:], in1=unit["gated"][:], op=ALU.add)
-            unit["pre_n"] = pre_n
+        def candidate_input(unit, cols=EVERY):
+            if "pre_n" not in unit:
+                pre_n = gating.tile([P, CHUNK], F32)
+                unit["pre_n"] = pre_n
+            nc.vector.tensor_tensor(
+                out=unit["pre_n"][:, cols], in0=unit["acc_in"][:, cols], in1=unit["gated"][:, cols], op=ALU.add
+            )
 
-        def candidate(unit):
+        def candidate(unit, cols=EVERY):
             pair, chunk, e = unit["where"]
-            n = gating.tile([P, CHUNK], F32)
-            nc.scalar.activation(out=n[:], in_=unit["pre_n"][:], func=ACT.Tanh, bias=bias_column(bias_in, 2, pair, e))
-            unit["n"] = n
+            if "n" not in unit:
+                n = gating.tile([P, CHUNK], F32)
+                unit["n"] = n
+            nc.scalar.activation(
+                out=unit["n"][:, cols],
+                in_=unit["pre_n"][:, cols],
+                func=ACT.Tanh,
+                bias=bias_column(bias_in, 2, pair, e),
+            )
 
 
-        def difference(unit, engine):
+        def difference(unit, engine, cols=EVERY):
             pair, chunk, e = unit["where"]
             state_t = x_grouped[chunk][:].rearrange("p (g b t) -> p g b t", g=PASSES, t=4)[
-                :, 1 + pair // 2, :, 2 * (pair % 2) + e
+                :, 1 + pair // 2, cols, 2 * (pair % 2) + e
             ]
-            away = apart.tile([P, CHUNK], F32)
-            engine.tensor_tensor(out=away[:], in0=unit["n"][:], in1=state_t, op=ALU.subtract)
-            unit["away"] = away
+            if "away" not in unit:
+                away = apart.tile([P, CHUNK], F32)
+                unit["away"] = away
+            engine.tensor_tensor(out=unit["away"][:, cols], in0=unit["n"][:, cols], in1=state_t, op=ALU.subtract)
 
-        def change(unit):
-            change_t = changes.tile([P, CHUNK], F32)
-            nc.vector.tensor_tensor(out=change_t[:], in0=unit["one_minus_z"][:], in1=unit["away"][:], op=ALU.mult)
-            change_tiles[unit["where"]] = change_t
+        def change(unit, cols=EVERY):
+            if unit["where"] not in change_tiles:
+                change_t = changes.tile([P, CHUNK], F32)
+                change_tiles[unit["where"]] = change_t
+            nc.vector.tensor_tensor(
+                out=change_tiles[unit["where"]][:, cols],
+                in0=unit["one_minus_z"][:, cols],
+                in1=unit["away"][:, cols],
+                op=ALU.mult,
+            )
 
         change_tiles = {}
 
@@ -290,19 +299,12 @@ def tile_rssm_pb_kernel(tc, sample, prev_action, prev_state, gru_Wih, gru_Whh, g
         ident = const.tile([P, P], F32)
         make_identity(nc, ident[:])
 
-        shared = [nc.scalar.copy, nc.scalar.copy, nc.vector.tensor_copy]
-        scalar_only = [nc.scalar.copy, nc.scalar.copy, nc.scalar.copy]
-
         load_x(0)
         for gate in range(GATES):
             load_w(0, gate)
         load_x(1)
         for gate in range(GATES):
             load_w(1, gate)
-
-        for half in range(2):
-            flip_x(0, half, shared)
-            quantise_x(0, half)
 
         bias_tile = next_bank()
         bias_bank = bias_tile[:].rearrange("p a u r -> p (a u r)")
@@ -312,35 +314,62 @@ def tile_rssm_pb_kernel(tc, sample, prev_action, prev_state, gru_Wih, gru_Whh, g
         bias_in = bias_all[:, 0 : 2 * n_rows]
         bias_hid = bias_all[:, 2 * n_rows : 4 * n_rows]
         bias_both = const.tile([P, 2 * n_rows], F32)
-        nc.vector.tensor_tensor(out=bias_both[:], in0=bias_in, in1=bias_hid, op=ALU.add)
+        nc.gpsimd.tensor_tensor(out=bias_both[:], in0=bias_in, in1=bias_hid, op=ALU.add)
         bias_both_negative = const.tile([P, 2 * n_rows], F32)
-        nc.vector.tensor_scalar_mul(out=bias_both_negative[:], in0=bias_both[:], scalar1=-1.0)
+        nc.gpsimd.tensor_scalar(out=bias_both_negative[:], in0=bias_both[:], scalar1=-1.0, scalar2=None, op0=ALU.mult)
+
+        act = nc.scalar.copy
+        vec = nc.vector.tensor_copy
+
+        flip_x(0, 0, 0, act)
+        flip_x(0, 1, 0, vec)
+        quantise_x(0, 0, 0)
+        flip_x(0, 0, 1, act)
+        flip_x(0, 0, 2, act)
+        quantise_x(0, 1, 0)
+        quantise_x(0, 0, 1)
+        flip_x(0, 1, 1, vec)
+        flip_x(0, 1, 2, act)
+        quantise_x(0, 0, 2)
+        quantise_x(0, 1, 1)
+        quantise_x(0, 1, 2)
 
         first_units = [{"where": (0, 0, 0)}, {"where": (0, 0, 1)}]
-        flip_w(0, 0, shared, lambda g: next_bank())
-        quantise_w(0, 0)
-        flip_w(0, 1, shared, lambda g: next_bank())
-        quantise_w(0, 1)
+        shares = [act, vec, act]
+        for gate in range(2):
+            for g in range(PASSES):
+                flip_w(0, gate, g, shares[g], next_bank())
+            for g in range(PASSES):
+                quantise_w(0, gate, g)
         for unit in first_units:
             reset_gate(unit)
-        flip_w(0, 2, shared, lambda g: next_bank())
-        quantise_w(0, 2)
+        for g in range(PASSES):
+            flip_w(0, 2, g, shares[g], next_bank())
+        for g in range(PASSES):
+            quantise_w(0, 2, g)
         for unit in first_units:
             update_gate(unit)
+        for g in range(PASSES):
+            flip_x(1, 0, g, act)
+        for g in range(PASSES):
+            quantise_x(1, 0, g)
         for unit in first_units:
             candidate_sums(unit)
             gate_hidden(unit)
         for unit in first_units:
             candidate_input(unit)
-        for half in range(2):
-            flip_x(1, half, shared)
-            quantise_x(1, half)
-        flip_w(1, 0, shared, lambda g: next_bank())
+        for g in range(PASSES):
+            flip_x(1, 1, g, act)
+        for g in range(PASSES):
+            quantise_x(1, 1, g)
         for unit in first_units:
             candidate(unit)
         difference(first_units[0], nc.gpsimd)
+        for g in range(PASSES):
+            flip_w(1, 0, g, act, next_bank())
         load_w(2, 0)
-        quantise_w(1, 0)
+        for g in range(PASSES):
+            quantise_w(1, 0, g)
         change(first_units[0])
         previous = first_units[1]
 
@@ -350,7 +379,7 @@ def tile_rssm_pb_kernel(tc, sample, prev_action, prev_state, gru_Wih, gru_Whh, g
 
 
         waiting = []
-        for rnd in range(2, ROUNDS):
+        for rnd in range(2, ROUNDS - 1):
             pair, step = divmod(rnd, 2 * CHUNKS)
             chunk, e = divmod(step, 2)
             more_weights = pair + 1 < PAIRS and step > 0
@@ -360,28 +389,45 @@ def tile_rssm_pb_kernel(tc, sample, prev_action, prev_state, gru_Wih, gru_Whh, g
             update_gate(unit)
             candidate_sums(unit)
             difference(previous, nc.gpsimd)
-            gate_hidden(unit)
             for bank_number, bank in waiting:
                 add_state_and_store(bank_number, bank)
             waiting = []
+            gate_hidden(unit)
             candidate_input(unit)
             if more_weights:
-                flip_w(pair + 1, step - 1, scalar_only, weight_bank)
+                for g in range(PASSES):
+                    flip_w(pair + 1, step - 1, g, act, weight_bank(g))
             candidate(unit)
             if rnd >= RETURN_LAG:
                 waiting.append((rnd - RETURN_LAG, flip_results(rnd - RETURN_LAG)))
             if pair + 2 < PAIRS and step > 0:
                 load_w(pair + 2, step - 1)
             if more_weights:
-                quantise_w(pair + 1, step - 1)
+                for g in range(PASSES):
+                    quantise_w(pair + 1, step - 1, g)
             change(previous)
             previous = unit
 
-        waiting.append((ROUNDS - RETURN_LAG, flip_results(ROUNDS - RETURN_LAG, 2)))
-        difference(previous, nc.vector)
+
+        unit = {"where": (PAIRS - 1, CHUNKS - 1, 1)}
+        reset_gate(unit)
+        candidate_sums(unit)
+        update_gate(unit)
+        difference(previous, nc.gpsimd)
         for bank_number, bank in waiting:
             add_state_and_store(bank_number, bank)
+        for cols in HALVES:
+            gate_hidden(unit, cols)
+        for cols in HALVES:
+            candidate_input(unit, cols)
+            candidate(unit, cols)
+        waiting = [(number, flip_results(number, number % 3)) for number in range(ROUNDS - 1 - RETURN_LAG, ROUNDS - 2)]
         change(previous)
-        for bank_number in range(ROUNDS - RETURN_LAG + 1, ROUNDS):
-            bank = flip_results(bank_number, bank_number % 2)
+        for cols in HALVES:
+            difference(unit, nc.vector, cols)
+        last = []
+        for half in range(2):
+            change(unit, HALVES[half])
+            last.append((ROUNDS - 2 + half, flip_results(ROUNDS - 2 + half, 2 + half)))
+        for bank_number, bank in waiting + last:
             add_state_and_store(bank_number, bank)

@@ -306,18 +306,6 @@ def tile_rssm_pb_kernel(tc, sample, prev_action, prev_state, gru_Wih, gru_Whh, g
         for gate in range(GATES):
             load_w(1, gate)
 
-        bias_tile = next_bank()
-        bias_bank = bias_tile[:].rearrange("p a u r -> p (a u r)")
-        nc.tensor.transpose(bias_bank[:, 0:P], bias_rows[:].bitcast(F32), ident[:])
-        bias_all = const.tile([P, 4 * n_rows], F32)
-        nc.vector.tensor_copy(out=bias_all[:], in_=bias_bank.bitcast(BF16)[:, 0 : 4 * n_rows])
-        bias_in = bias_all[:, 0 : 2 * n_rows]
-        bias_hid = bias_all[:, 2 * n_rows : 4 * n_rows]
-        bias_both = const.tile([P, 2 * n_rows], F32)
-        nc.gpsimd.tensor_tensor(out=bias_both[:], in0=bias_in, in1=bias_hid, op=ALU.add)
-        bias_both_negative = const.tile([P, 2 * n_rows], F32)
-        nc.gpsimd.tensor_scalar(out=bias_both_negative[:], in0=bias_both[:], scalar1=-1.0, scalar2=None, op0=ALU.mult)
-
         act = nc.scalar.copy
         vec = nc.vector.tensor_copy
 
@@ -336,11 +324,27 @@ def tile_rssm_pb_kernel(tc, sample, prev_action, prev_state, gru_Wih, gru_Whh, g
 
         first_units = [{"where": (0, 0, 0)}, {"where": (0, 0, 1)}]
         shares = [act, vec, act]
-        for gate in range(2):
-            for g in range(PASSES):
-                flip_w(0, gate, g, shares[g], next_bank())
-            for g in range(PASSES):
-                quantise_w(0, gate, g)
+        for g in range(PASSES):
+            flip_w(0, 0, g, shares[g], next_bank())
+        for g in range(PASSES):
+            quantise_w(0, 0, g)
+
+        bias_tile = next_bank()
+        bias_bank = bias_tile[:].rearrange("p a u r -> p (a u r)")
+        nc.tensor.transpose(bias_bank[:, 0:P], bias_rows[:].bitcast(F32), ident[:])
+        bias_all = const.tile([P, 4 * n_rows], F32)
+        nc.vector.tensor_copy(out=bias_all[:], in_=bias_bank.bitcast(BF16)[:, 0 : 4 * n_rows])
+        bias_in = bias_all[:, 0 : 2 * n_rows]
+        bias_hid = bias_all[:, 2 * n_rows : 4 * n_rows]
+        bias_both = const.tile([P, 2 * n_rows], F32)
+        nc.gpsimd.tensor_tensor(out=bias_both[:], in0=bias_in, in1=bias_hid, op=ALU.add)
+        bias_both_negative = const.tile([P, 2 * n_rows], F32)
+        nc.gpsimd.tensor_scalar(out=bias_both_negative[:], in0=bias_both[:], scalar1=-1.0, scalar2=None, op0=ALU.mult)
+
+        for g in range(PASSES):
+            flip_w(0, 1, g, shares[g], next_bank())
+        for g in range(PASSES):
+            quantise_w(0, 1, g)
         for unit in first_units:
             reset_gate(unit)
         for g in range(PASSES):

@@ -377,16 +377,27 @@ def tile_rssm_pb_kernel(tc, sample, prev_action, prev_state, gru_Wih, gru_Whh, g
         change(first_units[0])
         previous = first_units[1]
 
-        def weight_bank(g):
-            bank = flipped.tile([P, 2, 2, P], F32, tag="bank" + str(g))
+        weight_banks_taken = [0]
+
+        def weight_bank():
+            bank = flipped.tile([P, 2, 2, P], F32, tag="bank" + str(weight_banks_taken[0] % 3))
+            weight_banks_taken[0] += 1
             return bank
+
+        in_order = [(0, 0), (0, 1), (0, 2), (1, 0), (1, 1), (1, 2), (2, 1), (2, 2), (2, 0)]
+        weight_rounds = {2: in_order[3:6], 3: in_order[6:9]}
+        for pair in range(1, PAIRS - 1):
+            first_round = pair * 2 * CHUNKS
+            weight_rounds[first_round] = in_order[0:3]
+            for step in range(1, 2 * CHUNKS):
+                weight_rounds[first_round + step] = in_order[2 * step + 1 : 2 * step + 3]
 
 
         waiting = []
         for rnd in range(2, ROUNDS - 1):
             pair, step = divmod(rnd, 2 * CHUNKS)
             chunk, e = divmod(step, 2)
-            more_weights = pair + 1 < PAIRS and step > 0
+            next_banks = weight_rounds.get(rnd, [])
 
             unit = {"where": (pair, chunk, e)}
             reset_gate(unit)
@@ -398,17 +409,15 @@ def tile_rssm_pb_kernel(tc, sample, prev_action, prev_state, gru_Wih, gru_Whh, g
             waiting = []
             gate_hidden(unit)
             candidate_input(unit)
-            if more_weights:
-                for g in range(PASSES):
-                    flip_w(pair + 1, step - 1, g, act, weight_bank(g))
+            for gate, g in next_banks:
+                flip_w(pair + 1, gate, g, act, weight_bank())
             candidate(unit)
             if rnd >= RETURN_LAG:
                 waiting.append((rnd - RETURN_LAG, flip_results(rnd - RETURN_LAG)))
             if pair + 2 < PAIRS and step > 0:
                 load_w(pair + 2, step - 1)
-            if more_weights:
-                for g in range(PASSES):
-                    quantise_w(pair + 1, step - 1, g)
+            for gate, g in next_banks:
+                quantise_w(pair + 1, gate, g)
             change(previous)
             previous = unit
 

@@ -202,9 +202,12 @@ def tile_rssm_pb_kernel(tc, sample, prev_action, prev_state, gru_Wih, gru_Whh, g
             )
             unit["one_minus_z"] = one_minus_z
 
-        def candidate_sums(unit):
+        def hidden_sums(unit):
             pair, chunk, e = unit["where"]
             unit["acc_hn"] = mx_group(pair, chunk, e, 2, [1, 2])
+
+        def input_sums(unit):
+            pair, chunk, e = unit["where"]
             unit["acc_in"] = mx_group(pair, chunk, e, 2, [0])
 
         def gate_hidden(unit, cols=EVERY):
@@ -309,15 +312,28 @@ def tile_rssm_pb_kernel(tc, sample, prev_action, prev_state, gru_Wih, gru_Whh, g
         act = nc.scalar.copy
         vec = nc.vector.tensor_copy
 
+        zeros = const.tile([P, CHUNK], BF16)
+        nc.vector.memset(zeros[:], 0.0)
+
+        def keep_clock(count):
+            for number in range(count):
+                unread = sums.tile([P, CHUNK], F32, tag="acc")
+                nc.tensor.matmul(out=unread[:], lhsT=zeros[:, 0:P], rhs=zeros[:], start=True, stop=True)
+
+        keep_clock(5)
+
         flip_x(0, 0, 0, act)
         flip_x(0, 1, 0, vec)
+        keep_clock(1)
         quantise_x(0, 0, 0)
         flip_x(0, 0, 1, act)
         flip_x(0, 0, 2, act)
+        keep_clock(1)
         quantise_x(0, 1, 0)
         quantise_x(0, 0, 1)
         flip_x(0, 1, 1, vec)
         flip_x(0, 1, 2, act)
+        keep_clock(2)
         quantise_x(0, 0, 2)
         quantise_x(0, 1, 1)
         quantise_x(0, 1, 2)
@@ -326,6 +342,7 @@ def tile_rssm_pb_kernel(tc, sample, prev_action, prev_state, gru_Wih, gru_Whh, g
         shares = [act, vec, act]
         for g in range(PASSES):
             flip_w(0, 0, g, shares[g], next_bank())
+        keep_clock(1)
         for g in range(PASSES):
             quantise_w(0, 0, g)
 
@@ -343,6 +360,7 @@ def tile_rssm_pb_kernel(tc, sample, prev_action, prev_state, gru_Wih, gru_Whh, g
 
         for g in range(PASSES):
             flip_w(0, 1, g, shares[g], next_bank())
+        keep_clock(1)
         for g in range(PASSES):
             quantise_w(0, 1, g)
         for unit in first_units:
@@ -358,19 +376,21 @@ def tile_rssm_pb_kernel(tc, sample, prev_action, prev_state, gru_Wih, gru_Whh, g
         for g in range(PASSES):
             quantise_x(1, 0, g)
         for unit in first_units:
-            candidate_sums(unit)
+            hidden_sums(unit)
             gate_hidden(unit)
-        for unit in first_units:
-            candidate_input(unit)
         for g in range(PASSES):
             flip_x(1, 1, g, act)
+        for unit in first_units:
+            input_sums(unit)
         for g in range(PASSES):
             quantise_x(1, 1, g)
         for unit in first_units:
-            candidate(unit)
-        difference(first_units[0], nc.gpsimd)
+            candidate_input(unit)
         for g in range(PASSES):
             flip_w(1, 0, g, act, next_bank())
+        for unit in first_units:
+            candidate(unit)
+        difference(first_units[0], nc.gpsimd)
         load_w(2, 0)
         for g in range(PASSES):
             quantise_w(1, 0, g)
@@ -402,7 +422,8 @@ def tile_rssm_pb_kernel(tc, sample, prev_action, prev_state, gru_Wih, gru_Whh, g
             unit = {"where": (pair, chunk, e)}
             reset_gate(unit)
             update_gate(unit)
-            candidate_sums(unit)
+            hidden_sums(unit)
+            input_sums(unit)
             difference(previous, nc.gpsimd)
             for bank_number, bank in waiting:
                 add_state_and_store(bank_number, bank)
@@ -424,7 +445,8 @@ def tile_rssm_pb_kernel(tc, sample, prev_action, prev_state, gru_Wih, gru_Whh, g
 
         unit = {"where": (PAIRS - 1, CHUNKS - 1, 1)}
         reset_gate(unit)
-        candidate_sums(unit)
+        hidden_sums(unit)
+        input_sums(unit)
         update_gate(unit)
         difference(previous, nc.gpsimd)
         for bank_number, bank in waiting:

@@ -100,16 +100,17 @@ def tile_rssm_pb_kernel(tc, sample, prev_action, prev_state, gru_Wih, gru_Whh, g
             x_codes.append(codes)
             x_scales.append(scales)
 
-        def load_x(chunk):
-            tiles = slice(chunk * CHUNK_TILES, (chunk + 1) * CHUNK_TILES)
+        def load_x(chunk, first, count):
+            here = slice(first, first + count)
+            there = slice(chunk * CHUNK_TILES + first, chunk * CHUNK_TILES + first + count)
             in_view = x_in_rows[chunk][:].rearrange("p (t k) -> p t k", t=CHUNK_TILES)
+            nc.sync.dma_start(out=in_view[:, here, 0:LATENT], in_=sample_v[:, there, :])
+            nc.sync.dma_start(out=in_view[:, here, LATENT:K_IN], in_=action_v[:, there, :])
+
+        def load_state(chunk, half):
             hid_view = x_hid_rows[chunk][:].rearrange("p (t k) -> p t k", t=CHUNK_TILES)
-            nc.sync.dma_start(out=in_view[:, :, 0:LATENT], in_=sample_v[:, tiles, :])
-            nc.sync.dma_start(out=in_view[:, :, LATENT:K_IN], in_=action_v[:, tiles, :])
-            for half in range(2):
-                pair_of_tiles = slice(2 * half, 2 * half + 2)
-                first_tile = chunk * CHUNK_TILES + 2 * half
-                nc.sync.dma_start(out=hid_view[:, pair_of_tiles, :], in_=state_v[:, first_tile : first_tile + 2, :])
+            first = chunk * CHUNK_TILES + 2 * half
+            nc.sync.dma_start(out=hid_view[:, 2 * half : 2 * half + 2, :], in_=state_v[:, first : first + 2, :])
 
         def flip_x(chunk, half, g, copy_out):
             start = (g * CHUNK + half * 2 * P) * 2
@@ -161,18 +162,20 @@ def tile_rssm_pb_kernel(tc, sample, prev_action, prev_state, gru_Wih, gru_Whh, g
             w_ready[(pair, gate, g)] = (w_codes, w_scales)
 
 
-        def mx_group(pair, chunk, e, gate, passes):
-            acc = sums.tile([P, CHUNK], F32, tag="acc")
+        def mx_group(unit, gate, passes, cols, acc=None):
+            pair, chunk, e = unit["where"]
+            if acc is None:
+                acc = sums.tile([P, CHUNK], F32, tag="acc")
             units = slice(e * P, (e + 1) * P)
             for g in passes:
                 w_codes, w_scales = w_ready[(pair, gate, g)]
-                cols = slice(g * CHUNK, (g + 1) * CHUNK)
+                moving = slice(g * CHUNK + cols.start, g * CHUNK + cols.stop)
                 nc.tensor.matmul_mx(
-                    out=acc[:],
+                    out=acc[:, cols],
                     lhsT=w_codes[:, units].bitcast(FP8X4),
                     lhsT_scale=w_scales[:, units],
-                    rhs=x_codes[chunk][:, cols].bitcast(FP8X4),
-                    rhs_scale=x_scales[chunk][:, cols],
+                    rhs=x_codes[chunk][:, moving].bitcast(FP8X4),
+                    rhs_scale=x_scales[chunk][:, moving],
                     start=(g == passes[0]),
                     stop=(g == passes[-1]),
                 )
@@ -182,33 +185,35 @@ def tile_rssm_pb_kernel(tc, sample, prev_action, prev_state, gru_Wih, gru_Whh, g
             column = (gate * PAIRS + pair) * 2 + e
             return table[:, column : column + 1]
 
-        def reset_gate(unit):
+        def reset_gate(unit, cols=EVERY):
             pair, chunk, e = unit["where"]
-            acc_r = mx_group(pair, chunk, e, 0, [0, 1, 2])
-            r = gating.tile([P, CHUNK], F32)
-            nc.scalar.activation(out=r[:], in_=acc_r[:], func=ACT.Sigmoid, bias=bias_column(bias_both, 0, pair, e))
-            unit["r"] = r
-
-        def update_gate(unit):
-            pair, chunk, e = unit["where"]
-            acc_z = mx_group(pair, chunk, e, 1, [0, 1, 2])
-            one_minus_z = gating.tile([P, CHUNK], F32)
+            acc_r = mx_group(unit, 0, [0, 1, 2], cols)
+            if "r" not in unit:
+                r = gating.tile([P, CHUNK], F32)
+                unit["r"] = r
             nc.scalar.activation(
-                out=one_minus_z[:],
-                in_=acc_z[:],
+                out=unit["r"][:, cols], in_=acc_r[:, cols], func=ACT.Sigmoid, bias=bias_column(bias_both, 0, pair, e)
+            )
+
+        def update_gate(unit, cols=EVERY, acc=None):
+            pair, chunk, e = unit["where"]
+            acc_z = mx_group(unit, 1, [0, 1, 2], cols, acc)
+            if "one_minus_z" not in unit:
+                one_minus_z = gating.tile([P, CHUNK], F32)
+                unit["one_minus_z"] = one_minus_z
+            nc.scalar.activation(
+                out=unit["one_minus_z"][:, cols],
+                in_=acc_z[:, cols],
                 func=ACT.Sigmoid,
                 bias=bias_column(bias_both_negative, 1, pair, e),
                 scale=-1.0,
             )
-            unit["one_minus_z"] = one_minus_z
 
-        def hidden_sums(unit):
-            pair, chunk, e = unit["where"]
-            unit["acc_hn"] = mx_group(pair, chunk, e, 2, [1, 2])
+        def hidden_sums(unit, cols=EVERY):
+            unit["acc_hn"] = mx_group(unit, 2, [1, 2], cols)
 
-        def input_sums(unit):
-            pair, chunk, e = unit["where"]
-            unit["acc_in"] = mx_group(pair, chunk, e, 2, [0])
+        def input_sums(unit, cols=EVERY):
+            unit["acc_in"] = mx_group(unit, 2, [0], cols)
 
         def gate_hidden(unit, cols=EVERY):
             pair, chunk, e = unit["where"]
@@ -255,11 +260,11 @@ def tile_rssm_pb_kernel(tc, sample, prev_action, prev_state, gru_Wih, gru_Whh, g
                 unit["away"] = away
             engine.tensor_tensor(out=unit["away"][:, cols], in0=unit["n"][:, cols], in1=state_t, op=ALU.subtract)
 
-        def change(unit, cols=EVERY):
+        def change(unit, engine, cols=EVERY):
             if unit["where"] not in change_tiles:
                 change_t = changes.tile([P, CHUNK], F32)
                 change_tiles[unit["where"]] = change_t
-            nc.vector.tensor_tensor(
+            engine.tensor_tensor(
                 out=change_tiles[unit["where"]][:, cols],
                 in0=unit["one_minus_z"][:, cols],
                 in1=unit["away"][:, cols],
@@ -302,10 +307,16 @@ def tile_rssm_pb_kernel(tc, sample, prev_action, prev_state, gru_Wih, gru_Whh, g
         ident = const.tile([P, P], F32)
         make_identity(nc, ident[:])
 
-        load_x(0)
-        for gate in range(GATES):
+        load_x(0, 0, 2)
+        load_state(0, 0)
+        load_w(0, 0)
+        load_x(0, 2, 2)
+        load_state(0, 1)
+        for gate in range(1, GATES):
             load_w(0, gate)
-        load_x(1)
+        load_x(1, 0, CHUNK_TILES)
+        for half in range(2):
+            load_state(1, half)
         for gate in range(GATES):
             load_w(1, gate)
 
@@ -322,30 +333,26 @@ def tile_rssm_pb_kernel(tc, sample, prev_action, prev_state, gru_Wih, gru_Whh, g
 
         keep_clock(5)
 
-        flip_x(0, 0, 0, act)
-        flip_x(0, 1, 0, vec)
-        keep_clock(1)
-        quantise_x(0, 0, 0)
-        flip_x(0, 0, 1, act)
-        flip_x(0, 0, 2, act)
-        keep_clock(1)
-        quantise_x(0, 1, 0)
-        quantise_x(0, 0, 1)
-        flip_x(0, 1, 1, vec)
-        flip_x(0, 1, 2, act)
-        keep_clock(2)
-        quantise_x(0, 0, 2)
-        quantise_x(0, 1, 1)
-        quantise_x(0, 1, 2)
-
         first_units = [{"where": (0, 0, 0)}, {"where": (0, 0, 1)}]
         shares = [act, vec, act]
-        for g in range(PASSES):
-            flip_w(0, 0, g, shares[g], next_bank())
+
+        flip_x(0, 0, 0, act)
+        keep_clock(1)
+        quantise_x(0, 0, 0)
+        flip_x(0, 0, 1, vec)
+        flip_x(0, 0, 2, act)
+        keep_clock(1)
+        flip_w(0, 0, 0, act, next_bank())
+        quantise_x(0, 0, 1)
+        quantise_x(0, 0, 2)
+        flip_w(0, 0, 1, vec, next_bank())
+        flip_w(0, 0, 2, act, next_bank())
         keep_clock(1)
         for g in range(PASSES):
             quantise_w(0, 0, g)
-
+        flip_x(0, 1, 0, act)
+        flip_x(0, 1, 1, vec)
+        flip_x(0, 1, 2, act)
         bias_tile = next_bank()
         bias_bank = bias_tile[:].rearrange("p a u r -> p (a u r)")
         nc.tensor.transpose(bias_bank[:, 0:P], bias_rows[:].bitcast(F32), ident[:])
@@ -358,13 +365,17 @@ def tile_rssm_pb_kernel(tc, sample, prev_action, prev_state, gru_Wih, gru_Whh, g
         bias_both_negative = const.tile([P, 2 * n_rows], F32)
         nc.gpsimd.tensor_scalar(out=bias_both_negative[:], in0=bias_both[:], scalar1=-1.0, scalar2=None, op0=ALU.mult)
 
+        for unit in first_units:
+            reset_gate(unit, HALVES[0])
         for g in range(PASSES):
-            flip_w(0, 1, g, shares[g], next_bank())
-        keep_clock(1)
+            quantise_x(0, 1, g)
+        flip_w(0, 1, 0, act, next_bank())
+        flip_w(0, 1, 1, vec, next_bank())
+        flip_w(0, 1, 2, act, next_bank())
+        for unit in first_units:
+            reset_gate(unit, HALVES[1])
         for g in range(PASSES):
             quantise_w(0, 1, g)
-        for unit in first_units:
-            reset_gate(unit)
         for g in range(PASSES):
             flip_w(0, 2, g, shares[g], next_bank())
         for g in range(PASSES):
@@ -394,7 +405,7 @@ def tile_rssm_pb_kernel(tc, sample, prev_action, prev_state, gru_Wih, gru_Whh, g
         load_w(2, 0)
         for g in range(PASSES):
             quantise_w(1, 0, g)
-        change(first_units[0])
+        change(first_units[0], nc.vector)
         previous = first_units[1]
 
         weight_banks_taken = [0]
@@ -413,11 +424,18 @@ def tile_rssm_pb_kernel(tc, sample, prev_action, prev_state, gru_Wih, gru_Whh, g
                 weight_rounds[first_round + step] = in_order[2 * step + 1 : 2 * step + 3]
 
 
+        return_rounds = {}
+        for rnd in range(RETURN_LAG, ROUNDS - 2 * CHUNKS):
+            return_rounds[rnd] = [rnd - RETURN_LAG]
+        return_rounds[12] = [9]
+        return_rounds[13] = [10, 11]
+        return_rounds[14] = []
         waiting = []
         for rnd in range(2, ROUNDS - 1):
             pair, step = divmod(rnd, 2 * CHUNKS)
             chunk, e = divmod(step, 2)
             next_banks = weight_rounds.get(rnd, [])
+            last_pair = pair == PAIRS - 1
 
             unit = {"where": (pair, chunk, e)}
             reset_gate(unit)
@@ -427,42 +445,60 @@ def tile_rssm_pb_kernel(tc, sample, prev_action, prev_state, gru_Wih, gru_Whh, g
             difference(previous, nc.gpsimd)
             for bank_number, bank in waiting:
                 add_state_and_store(bank_number, bank)
-            waiting = []
+            if last_pair:
+                change(previous, nc.gpsimd)
             gate_hidden(unit)
             candidate_input(unit)
             for gate, g in next_banks:
                 flip_w(pair + 1, gate, g, act, weight_bank())
-            candidate(unit)
-            if rnd >= RETURN_LAG:
-                waiting.append((rnd - RETURN_LAG, flip_results(rnd - RETURN_LAG)))
+            if rnd < ROUNDS - 2:
+                candidate(unit)
+            waiting = []
+            for bank_number in return_rounds.get(rnd, []):
+                waiting.append((bank_number, flip_results(bank_number, bank_number % 4 if last_pair else 3)))
             if pair + 2 < PAIRS and step > 0:
                 load_w(pair + 2, step - 1)
             for gate, g in next_banks:
                 quantise_w(pair + 1, gate, g)
-            change(previous)
+            if not last_pair:
+                change(previous, nc.vector)
             previous = unit
 
 
-        unit = {"where": (PAIRS - 1, CHUNKS - 1, 1)}
-        reset_gate(unit)
-        hidden_sums(unit)
-        input_sums(unit)
-        update_gate(unit)
-        difference(previous, nc.gpsimd)
+        last_away = apart.tile([P, CHUNK], F32)
+        unit = {"where": (PAIRS - 1, CHUNKS - 1, 1), "away": last_away}
+        left, right = HALVES
+        reset_gate(unit, left)
+        candidate(previous)
+        hidden_sums(unit, left)
+        input_sums(unit, left)
+        spare = flipped.tile([P, CHUNK], F32, tag="bank2")
+        update_gate(unit, left, spare)
         for bank_number, bank in waiting:
             add_state_and_store(bank_number, bank)
-        for cols in HALVES:
-            gate_hidden(unit, cols)
-        for cols in HALVES:
-            candidate_input(unit, cols)
-            candidate(unit, cols)
-        waiting = [(number, flip_results(number, number % 3)) for number in range(ROUNDS - 1 - RETURN_LAG, ROUNDS - 2)]
-        change(previous)
-        for cols in HALVES:
-            difference(unit, nc.vector, cols)
-        last = []
-        for half in range(2):
-            change(unit, HALVES[half])
-            last.append((ROUNDS - 2 + half, flip_results(ROUNDS - 2 + half, 2 + half)))
-        for bank_number, bank in waiting + last:
-            add_state_and_store(bank_number, bank)
+        gate_hidden(unit, left)
+        reset_gate(unit, right)
+        candidate_input(unit, left)
+        candidate(unit, left)
+        difference(previous, nc.vector)
+        hidden_sums(unit, right)
+        input_sums(unit, right)
+        update_gate(unit, right)
+        gate_hidden(unit, right)
+        difference(unit, nc.vector, left)
+        candidate_input(unit, right)
+        candidate(unit, right)
+        waiting = []
+        for bank_number in (ROUNDS - 4, ROUNDS - 3):
+            bank = flip_results(bank_number, bank_number % 2)
+            waiting.append(bank)
+        change(previous, nc.vector)
+        change(unit, nc.vector, left)
+        bank = flip_results(ROUNDS - 2, 2)
+        difference(unit, nc.vector, right)
+        add_state_and_store(ROUNDS - 4, waiting[0])
+        change(unit, nc.vector, right)
+        add_state_and_store(ROUNDS - 2, bank)
+        bank = flip_results(ROUNDS - 1, 3)
+        add_state_and_store(ROUNDS - 3, waiting[1])
+        add_state_and_store(ROUNDS - 1, bank)

@@ -337,12 +337,13 @@ def tile_rssm_pb_kernel(tc, sample, prev_action, prev_state, gru_Wih, gru_Whh, g
         shares = [act, vec, act]
 
         flip_x(0, 0, 0, act)
-        keep_clock(1)
+        keep_clock(2)
         quantise_x(0, 0, 0)
         flip_x(0, 0, 1, vec)
         flip_x(0, 0, 2, act)
         keep_clock(1)
         flip_w(0, 0, 0, act, next_bank())
+        keep_clock(1)
         quantise_x(0, 0, 1)
         quantise_x(0, 0, 2)
         flip_w(0, 0, 1, vec, next_bank())
@@ -351,6 +352,7 @@ def tile_rssm_pb_kernel(tc, sample, prev_action, prev_state, gru_Wih, gru_Whh, g
         for g in range(PASSES):
             quantise_w(0, 0, g)
         flip_x(0, 1, 0, act)
+        keep_clock(1)
         flip_x(0, 1, 1, vec)
         flip_x(0, 1, 2, act)
         bias_tile = next_bank()

@@ -283,20 +283,59 @@ def tile_rssm_pb_kernel(tc, sample, prev_action, prev_state, gru_Wih, gru_Whh, g
                     nc.tensor.transpose(bank[:, a, e, :], change_tiles[(pair, chunk, e)][:, cols], ident[:])
             return bank
 
-        def add_state_and_store(bank_number, bank):
+        def return_with_state(bank_number, bank_tag):
+            finished, half = divmod(bank_number, 2)
+            pair, chunk = divmod(finished, CHUNKS)
+            bank = flipped.tile([P, 2, 2, P], F32, tag="bank" + str(bank_tag))
+            state_rows = x_hid_rows[chunk][:].rearrange("p (t j q e) -> p t j q e", t=CHUNK_TILES, j=PAIRS, e=2)
+            for a in range(2):
+                tile_number = 2 * half + a
+                cols = slice(tile_number * P, (tile_number + 1) * P)
+                for e in range(2):
+                    nc.tensor.matmul(
+                        out=bank[:, a, e, :],
+                        lhsT=ident_bf16[:],
+                        rhs=state_rows[:, tile_number, pair, :, e],
+                        start=True,
+                        stop=False,
+                    )
+                    nc.tensor.matmul(
+                        out=bank[:, a, e, :],
+                        lhsT=change_tiles[(pair, chunk, e)][:, cols],
+                        rhs=ident[:],
+                        start=False,
+                        stop=True,
+                    )
+            return bank
+
+        def copy_and_store(bank_number, bank):
             finished, half = divmod(bank_number, 2)
             pair, chunk = divmod(finished, CHUNKS)
             units = slice(pair * PAIR, (pair + 1) * PAIR)
-            state_rows = x_hid_rows[chunk][:].rearrange("p (t h) -> p t h", t=CHUNK_TILES)[:, 2 * half : 2 * half + 2, units]
+            rows = results.tile([P, 2, PAIR], F32)
+            nc.scalar.copy(
+                out=rows[:].rearrange("p a (q e) -> p a q e", e=2), in_=bank[:].rearrange("p a e q -> p a q e")
+            )
+            first_tile = chunk * CHUNK_TILES + 2 * half
+            nc.sync.dma_start(out=out_v[:, first_tile : first_tile + 2, units], in_=rows[:])
+
+        def add_state_and_store(bank_number, bank, tiles=(0, 2)):
+            finished, half = divmod(bank_number, 2)
+            pair, chunk = divmod(finished, CHUNKS)
+            units = slice(pair * PAIR, (pair + 1) * PAIR)
+            first, end = tiles
+            state_rows = x_hid_rows[chunk][:].rearrange("p (t h) -> p t h", t=CHUNK_TILES)[
+                :, 2 * half + first : 2 * half + end, units
+            ]
             rows = results.tile([P, 2, PAIR], F32)
             nc.vector.tensor_tensor(
-                out=rows[:].rearrange("p a (q e) -> p a q e", e=2),
-                in0=bank[:].rearrange("p a e q -> p a q e"),
+                out=rows[:, first:end].rearrange("p a (q e) -> p a q e", e=2),
+                in0=bank[:, first:end].rearrange("p a e q -> p a q e"),
                 in1=state_rows.rearrange("p a (q e) -> p a q e", e=2),
                 op=ALU.add,
             )
             first_tile = chunk * CHUNK_TILES + 2 * half
-            nc.sync.dma_start(out=out_v[:, first_tile : first_tile + 2, units], in_=rows[:])
+            nc.sync.dma_start(out=out_v[:, first_tile + first : first_tile + end, units], in_=rows[:, first:end])
 
 
         bias_rows = const.tile([P, PAIR], BF16)
@@ -306,6 +345,8 @@ def tile_rssm_pb_kernel(tc, sample, prev_action, prev_state, gru_Wih, gru_Whh, g
         nc.scalar.dma_start(out=bias_rows[n_rows : 2 * n_rows, :], in_=gru_bhh.rearrange("(r w) -> r w", w=PAIR))
         ident = const.tile([P, P], F32)
         make_identity(nc, ident[:])
+        ident_bf16 = const.tile([P, P], BF16)
+        nc.gpsimd.tensor_copy(out=ident_bf16[:], in_=ident[:])
 
         load_x(0, 0, 2)
         load_state(0, 0)
@@ -429,9 +470,7 @@ def tile_rssm_pb_kernel(tc, sample, prev_action, prev_state, gru_Wih, gru_Whh, g
         return_rounds = {}
         for rnd in range(RETURN_LAG, ROUNDS - 2 * CHUNKS):
             return_rounds[rnd] = [rnd - RETURN_LAG]
-        return_rounds[12] = [9]
-        return_rounds[13] = [10, 11]
-        return_rounds[14] = []
+        return_rounds[13] = [9, 10, 11]
         waiting = []
         for rnd in range(2, ROUNDS - 1):
             pair, step = divmod(rnd, 2 * CHUNKS)
@@ -490,17 +529,16 @@ def tile_rssm_pb_kernel(tc, sample, prev_action, prev_state, gru_Wih, gru_Whh, g
         difference(unit, nc.vector, left)
         candidate_input(unit, right)
         candidate(unit, right)
-        waiting = []
-        for bank_number in (ROUNDS - 4, ROUNDS - 3):
-            bank = flip_results(bank_number, bank_number % 2)
-            waiting.append(bank)
+        bank_even = return_with_state(ROUNDS - 4, 0)
+        copy_and_store(ROUNDS - 4, bank_even)
+        bank_odd = flip_results(ROUNDS - 3, 1)
         change(previous, nc.vector)
         change(unit, nc.vector, left)
-        bank = flip_results(ROUNDS - 2, 2)
+        bank_left = flip_results(ROUNDS - 2, 2)
         difference(unit, nc.vector, right)
-        add_state_and_store(ROUNDS - 4, waiting[0])
+        add_state_and_store(ROUNDS - 3, bank_odd)
         change(unit, nc.vector, right)
-        add_state_and_store(ROUNDS - 2, bank)
-        bank = flip_results(ROUNDS - 1, 3)
-        add_state_and_store(ROUNDS - 3, waiting[1])
-        add_state_and_store(ROUNDS - 1, bank)
+        add_state_and_store(ROUNDS - 2, bank_left)
+        bank_right = flip_results(ROUNDS - 1, 3)
+        add_state_and_store(ROUNDS - 1, bank_right, (0, 1))
+        add_state_and_store(ROUNDS - 1, bank_right, (1, 2))

@@ -92,8 +92,8 @@ def tile_rssm_pb_kernel(tc, sample, prev_action, prev_state, gru_Wih, gru_Whh, g
             in_rows = x_keep.tile([P, CHUNK_TILES * K_IN], BF16)
             hid_rows = x_keep.tile([P, CHUNK_TILES * HIDDEN], BF16)
             grouped = x_keep.tile([P, PASSES * CHUNK * 4], BF16, align_bytes=64)
-            codes = x_keep.tile([P, PASSES * CHUNK], U32, align_bytes=64)
-            scales = x_keep.tile([P, PASSES * CHUNK], U8, align_bytes=64)
+            codes = x_keep.tile([P, PASSES * CHUNK], U32, align_bytes=256)
+            scales = x_keep.tile([P, PASSES * CHUNK], U8, align_bytes=256)
             x_in_rows.append(in_rows)
             x_hid_rows.append(hid_rows)
             x_grouped.append(grouped)
@@ -154,8 +154,8 @@ def tile_rssm_pb_kernel(tc, sample, prev_action, prev_state, gru_Wih, gru_Whh, g
             w_flipped[(pair, gate, g)] = w_pass
 
         def quantise_w(pair, gate, g):
-            w_codes = w_quant.tile([P, 2 * P], U32, align_bytes=64)
-            w_scales = w_quant.tile([P, 2 * P], U8, align_bytes=64)
+            w_codes = w_quant.tile([P, 2 * P], U32, align_bytes=256)
+            w_scales = w_quant.tile([P, 2 * P], U8, align_bytes=256)
             nc.vector.quantize_mx(
                 out=w_codes[:].bitcast(FP8X4), scales=w_scales[:], in_=w_flipped[(pair, gate, g)][:]
             )

from contextlib import ExitStack

import concourse.mybir as mybir
from concourse.masks import make_identity

F32 = mybir.dt.float32
BF16 = mybir.dt.bfloat16
U32 = mybir.dt.uint32
U8 = mybir.dt.uint8
FP8X4 = mybir.dt.float8_e4m3fn_x4
ACT = mybir.ActivationFunctionType
ALU = mybir.AluOpType

P = 128
BATCH = 1024
HIDDEN = 1024
LATENT = 384
K_IN = 512
GATES = 3
PASSES = 3
B_TILES = BATCH // P
CHUNK = 512
CHUNKS = BATCH // CHUNK
CHUNK_TILES = CHUNK // P
PAIR = 2 * P
PAIRS = HIDDEN // PAIR
ROUNDS = PAIRS * CHUNKS * 2
RETURN_LAG = 3
BANK_WORDS = 512

EVERY = slice(0, CHUNK)
HALVES = [slice(0, PAIR), slice(PAIR, 2 * PAIR)]

FLOPS = 2 * BATCH * GATES * HIDDEN * (K_IN + HIDDEN)


def tile_rssm_pb_kernel(tc, sample, prev_action, prev_state, gru_Wih, gru_Whh, gru_bih, gru_bhh, out):
    nc = tc.nc

    sample_v = sample.rearrange("(p t) k -> p t k", t=B_TILES)
    action_v = prev_action.rearrange("(p t) k -> p t k", t=B_TILES)
    state_v = prev_state.rearrange("(p t) k -> p t k", t=B_TILES)
    out_v = out.rearrange("(p t) h -> p t h", t=B_TILES)
    wih_v = gru_Wih.rearrange("(g j q e) k -> g j q (e k)", g=GATES, j=PAIRS, e=2)
    whh_v = gru_Whh.rearrange("(g j q e) k -> g j q (e k)", g=GATES, j=PAIRS, e=2)

    with ExitStack() as ctx:
        const = ctx.enter_context(tc.tile_pool(name="const", bufs=1))
        x_keep = ctx.enter_context(tc.tile_pool(name="x_keep", bufs=CHUNKS))
        w_rows = ctx.enter_context(tc.tile_pool(name="w_rows", bufs=2 * GATES))
        w_grouped = ctx.enter_context(tc.tile_pool(name="w_grouped", bufs=2 * PASSES))
        w_quant = ctx.enter_context(tc.tile_pool(name="w_quant", bufs=2 * GATES * PASSES))
        gating = ctx.enter_context(tc.tile_pool(name="gating", bufs=3))
        changes = ctx.enter_context(tc.tile_pool(name="changes", bufs=6))
        results = ctx.enter_context(tc.tile_pool(name="results", bufs=5))
        sums = ctx.enter_context(tc.psum_pool(name="sums", bufs=4))
        flipped = ctx.enter_context(tc.psum_pool(name="flipped", bufs=1))
        apart = ctx.enter_context(tc.tile_pool(name="apart", bufs=1))
        ctx.enter_context(tc.manual_schedule())


        banks_taken = [0]

        def next_bank():
            number = banks_taken[0] % 4
            banks_taken[0] += 1
            bank = flipped.tile([P, 2, 2, P], F32, tag="bank" + str(number))
            return bank

        def flip_pass(in_words, hid_words, rows, g, grouped_words, copy_out, bank):
            for a in range(2):
                for u in range(2):
                    if g == 0:
                        block = 2 * rows[a] + u
                        words = in_words[:, block * P : (block + 1) * P]
                    else:
                        block = 4 * rows[a] + 2 * (g - 1) + u
                        words = hid_words[:, block * P : (block + 1) * P]
                    nc.tensor.transpose(bank[:, a, u, :], words, ident[:])
            copy_out(
                out=grouped_words.rearrange("p (a r u) -> p a r u", a=2, u=2),
                in_=bank[:].rearrange("p a u r -> p a r u"),
            )


        x_in_rows = []
        x_hid_rows = []
        x_grouped = []
        x_codes = []
        x_scales = []
        for chunk in range(CHUNKS):
            in_rows = x_keep.tile([P, CHUNK_TILES * K_IN], BF16)
            hid_rows = x_keep.tile([P, CHUNK_TILES * HIDDEN], BF16)
            grouped = x_keep.tile([P, PASSES * CHUNK * 4], BF16, align_bytes=64)
            codes = x_keep.tile([P, PASSES * CHUNK], U32, align_bytes=256)
            scales = x_keep.tile([P, PASSES * CHUNK], U8, align_bytes=256)
            x_in_rows.append(in_rows)
            x_hid_rows.append(hid_rows)
            x_grouped.append(grouped)
            x_codes.append(codes)
            x_scales.append(scales)

        def load_x(chunk, first, count):
            here = slice(first, first + count)
            there = slice(chunk * CHUNK_TILES + first, chunk * CHUNK_TILES + first + count)
            in_view = x_in_rows[chunk][:].rearrange("p (t k) -> p t k", t=CHUNK_TILES)
            nc.sync.dma_start(out=in_view[:, here, 0:LATENT], in_=sample_v[:, there, :])
            nc.sync.dma_start(out=in_view[:, here, LATENT:K_IN], in_=action_v[:, there, :])

        def load_state(chunk, half):
            hid_view = x_hid_rows[chunk][:].rearrange("p (t k) -> p t k", t=CHUNK_TILES)
            first = chunk * CHUNK_TILES + 2 * half
            nc.sync.dma_start(out=hid_view[:, 2 * half : 2 * half + 2, :], in_=state_v[:, first : first + 2, :])

        def flip_x(chunk, half, g, copy_out):
            start = (g * CHUNK + half * 2 * P) * 2
            flip_pass(
                x_in_rows[chunk][:].bitcast(F32),
                x_hid_rows[chunk][:].bitcast(F32),
                [2 * half, 2 * half + 1],
                g,
                x_grouped[chunk][:].bitcast(F32)[:, start : start + BANK_WORDS],
                copy_out,
                next_bank(),
            )

        def quantise_x(chunk, half, g):
            first = g * CHUNK + half * 2 * P
            cols = slice(first, first + 2 * P)
            nc.vector.quantize_mx(
                out=x_codes[chunk][:, cols].bitcast(FP8X4),
                scales=x_scales[chunk][:, cols],
                in_=x_grouped[chunk][:, 4 * first : 4 * (first + 2 * P)],
            )


        w_loaded = {}
        w_flipped = {}
        w_ready = {}

        def load_w(pair, gate):
            wih_rows = w_rows.tile([P, 2 * K_IN], BF16)
            whh_rows = w_rows.tile([P, 2 * HIDDEN], BF16)
            nc.sync.dma_start(out=wih_rows[:], in_=wih_v[gate, pair])
            nc.sync.dma_start(out=whh_rows[:], in_=whh_v[gate, pair])
            w_loaded[(pair, gate)] = (wih_rows, whh_rows)

        def flip_w(pair, gate, g, copy_out, bank):
            wih_rows, whh_rows = w_loaded[(pair, gate)]
            w_pass = w_grouped.tile([P, 2 * P * 4], BF16, align_bytes=64)
            flip_pass(
                wih_rows[:].bitcast(F32), whh_rows[:].bitcast(F32), [0, 1], g, w_pass[:].bitcast(F32), copy_out, bank
            )
            w_flipped[(pair, gate, g)] = w_pass

        def quantise_w(pair, gate, g):
            w_codes = w_quant.tile([P, 2 * P], U32, align_bytes=256)
            w_scales = w_quant.tile([P, 2 * P], U8, align_bytes=256)
            nc.vector.quantize_mx(
                out=w_codes[:].bitcast(FP8X4), scales=w_scales[:], in_=w_flipped[(pair, gate, g)][:]
            )
            w_ready[(pair, gate, g)] = (w_codes, w_scales)


        def mx_group(unit, gate, passes, cols, acc=None):
            pair, chunk, e = unit["where"]
            if acc is None:
                acc = sums.tile([P, CHUNK], F32, tag="acc")
            units = slice(e * P, (e + 1) * P)
            for g in passes:
                w_codes, w_scales = w_ready[(pair, gate, g)]
                moving = slice(g * CHUNK + cols.start, g * CHUNK + cols.stop)
                nc.tensor.matmul_mx(
                    out=acc[:, cols],
                    lhsT=w_codes[:, units].bitcast(FP8X4),
                    lhsT_scale=w_scales[:, units],
                    rhs=x_codes[chunk][:, moving].bitcast(FP8X4),
                    rhs_scale=x_scales[chunk][:, moving],
                    start=(g == passes[0]),
                    stop=(g == passes[-1]),
                )
            return acc

        def bias_column(table, gate, pair, e):
            column = (gate * PAIRS + pair) * 2 + e
            return table[:, column : column + 1]

        def reset_gate(unit, cols=EVERY):
            pair, chunk, e = unit["where"]
            acc_r = mx_group(unit, 0, [0, 1, 2], cols)
            if "r" not in unit:
                r = gating.tile([P, CHUNK], F32)
                unit["r"] = r
            nc.scalar.activation(
                out=unit["r"][:, cols], in_=acc_r[:, cols], func=ACT.Sigmoid, bias=bias_column(bias_both, 0, pair, e)
            )

        def update_gate(unit, cols=EVERY, acc=None):
            pair, chunk, e = unit["where"]
            acc_z = mx_group(unit, 1, [0, 1, 2], cols, acc)
            if "one_minus_z" not in unit:
                one_minus_z = gating.tile([P, CHUNK], F32)
                unit["one_minus_z"] = one_minus_z
            nc.scalar.activation(
                out=unit["one_minus_z"][:, cols],
                in_=acc_z[:, cols],
                func=ACT.Sigmoid,
                bias=bias_column(bias_both_negative, 1, pair, e),
                scale=-1.0,
            )

        def hidden_sums(unit, cols=EVERY):
            unit["acc_hn"] = mx_group(unit, 2, [1, 2], cols)

        def input_sums(unit, cols=EVERY):
            unit["acc_in"] = mx_group(unit, 2, [0], cols)

        def gate_hidden(unit, cols=EVERY):
            pair, chunk, e = unit["where"]
            if "gated" not in unit:
                gated = gating.tile([P, CHUNK], F32)
                unit["gated"] = gated
            nc.vector.scalar_tensor_tensor(
                out=unit["gated"][:, cols],
                in0=unit["acc_hn"][:, cols],
                scalar=bias_column(bias_hid, 2, pair, e),
                in1=unit["r"][:, cols],
                op0=ALU.add,
                op1=ALU.mult,
            )

        def candidate_input(unit, cols=EVERY):
            if "pre_n" not in unit:
                pre_n = gating.tile([P, CHUNK], F32)
                unit["pre_n"] = pre_n
            nc.vector.tensor_tensor(
                out=unit["pre_n"][:, cols], in0=unit["acc_in"][:, cols], in1=unit["gated"][:, cols], op=ALU.add
            )

        def candidate(unit, cols=EVERY):
            pair, chunk, e = unit["where"]
            if "n" not in unit:
                n = gating.tile([P, CHUNK], F32)
                unit["n"] = n
            nc.scalar.activation(
                out=unit["n"][:, cols],
                in_=unit["pre_n"][:, cols],
                func=ACT.Tanh,
                bias=bias_column(bias_in, 2, pair, e),
            )


        def difference(unit, engine, cols=EVERY):
            pair, chunk, e = unit["where"]
            state_t = x_grouped[chunk][:].rearrange("p (g b t) -> p g b t", g=PASSES, t=4)[
                :, 1 + pair // 2, cols, 2 * (pair % 2) + e
            ]
            if "away" not in unit:
                away = apart.tile([P, CHUNK], F32)
                unit["away"] = away
            engine.tensor_tensor(out=unit["away"][:, cols], in0=unit["n"][:, cols], in1=state_t, op=ALU.subtract)

        def change(unit, engine, cols=EVERY):
            if unit["where"] not in change_tiles:
                change_t = changes.tile([P, CHUNK], F32)
                change_tiles[unit["where"]] = change_t
            engine.tensor_tensor(
                out=change_tiles[unit["where"]][:, cols],
                in0=unit["one_minus_z"][:, cols],
                in1=unit["away"][:, cols],
                op=ALU.mult,
            )

        change_tiles = {}

        def flip_results(bank_number, bank_tag=3):
            finished, half = divmod(bank_number, 2)
            pair, chunk = divmod(finished, CHUNKS)
            bank = flipped.tile([P, 2, 2, P], F32, tag="bank" + str(bank_tag))
            for a in range(2):
                cols = slice((2 * half + a) * P, (2 * half + a + 1) * P)
                for e in range(2):
                    nc.tensor.transpose(bank[:, a, e, :], change_tiles[(pair, chunk, e)][:, cols], ident[:])
            return bank

        def return_with_state(bank_number, bank_tag):
            finished, half = divmod(bank_number, 2)
            pair, chunk = divmod(finished, CHUNKS)
            bank = flipped.tile([P, 2, 2, P], F32, tag="bank" + str(bank_tag))
            state_rows = x_hid_rows[chunk][:].rearrange("p (t j q e) -> p t j q e", t=CHUNK_TILES, j=PAIRS, e=2)
            for a in range(2):
                tile_number = 2 * half + a
                cols = slice(tile_number * P, (tile_number + 1) * P)
                for e in range(2):
                    nc.tensor.matmul(
                        out=bank[:, a, e, :],
                        lhsT=ident_bf16[:],
                        rhs=state_rows[:, tile_number, pair, :, e],
                        start=True,
                        stop=False,
                    )
                    nc.tensor.matmul(
                        out=bank[:, a, e, :],
                        lhsT=change_tiles[(pair, chunk, e)][:, cols],
                        rhs=ident[:],
                        start=False,
                        stop=True,
                    )
            return bank

        def copy_and_store(bank_number, bank):
            finished, half = divmod(bank_number, 2)
            pair, chunk = divmod(finished, CHUNKS)
            units = slice(pair * PAIR, (pair + 1) * PAIR)
            rows = results.tile([P, 2, PAIR], F32)
            nc.scalar.copy(
                out=rows[:].rearrange("p a (q e) -> p a q e", e=2), in_=bank[:].rearrange("p a e q -> p a q e")
            )
            first_tile = chunk * CHUNK_TILES + 2 * half
            nc.sync.dma_start(out=out_v[:, first_tile : first_tile + 2, units], in_=rows[:])

        def add_state_and_store(bank_number, bank, tiles=(0, 2)):
            finished, half = divmod(bank_number, 2)
            pair, chunk = divmod(finished, CHUNKS)
            units = slice(pair * PAIR, (pair + 1) * PAIR)
            first, end = tiles
            state_rows = x_hid_rows[chunk][:].rearrange("p (t h) -> p t h", t=CHUNK_TILES)[
                :, 2 * half + first : 2 * half + end, units
            ]
            rows = results.tile([P, 2, PAIR], F32)
            nc.vector.tensor_tensor(
                out=rows[:, first:end].rearrange("p a (q e) -> p a q e", e=2),
                in0=bank[:, first:end].rearrange("p a e q -> p a q e"),
                in1=state_rows.rearrange("p a (q e) -> p a q e", e=2),
                op=ALU.add,
            )
            first_tile = chunk * CHUNK_TILES + 2 * half
            nc.sync.dma_start(out=out_v[:, first_tile + first : first_tile + end, units], in_=rows[:, first:end])


        bias_rows = const.tile([P, PAIR], BF16)
        nc.vector.memset(bias_rows[:], 0.0)
        n_rows = GATES * PAIRS
        nc.scalar.dma_start(out=bias_rows[0:n_rows, :], in_=gru_bih.rearrange("(r w) -> r w", w=PAIR))
        nc.scalar.dma_start(out=bias_rows[n_rows : 2 * n_rows, :], in_=gru_bhh.rearrange("(r w) -> r w", w=PAIR))
        ident = const.tile([P, P], F32)
        make_identity(nc, ident[:])
        ident_bf16 = const.tile([P, P], BF16)
        nc.gpsimd.tensor_copy(out=ident_bf16[:], in_=ident[:])

        load_x(0, 0, 2)
        load_state(0, 0)
        load_w(0, 0)
        load_x(0, 2, 2)
        load_state(0, 1)
        for gate in range(1, GATES):
            load_w(0, gate)
        load_x(1, 0, CHUNK_TILES)
        for half in range(2):
            load_state(1, half)
        for gate in range(GATES):
            load_w(1, gate)

        act = nc.scalar.copy
        vec = nc.vector.tensor_copy

        zeros = const.tile([P, CHUNK], BF16)
        nc.vector.memset(zeros[:], 0.0)

        def keep_clock(count):
            for number in range(count):
                unread = sums.tile([P, CHUNK], F32, tag="acc")
                nc.tensor.matmul(out=unread[:], lhsT=zeros[:, 0:P], rhs=zeros[:], start=True, stop=True)

        keep_clock(5)

        first_units = [{"where": (0, 0, 0)}, {"where": (0, 0, 1)}]
        shares = [act, vec, act]

        flip_x(0, 0, 0, act)
        keep_clock(2)
        quantise_x(0, 0, 0)
        flip_x(0, 0, 1, vec)
        flip_x(0, 0, 2, act)
        keep_clock(1)
        flip_w(0, 0, 0, act, next_bank())
        keep_clock(1)
        quantise_x(0, 0, 1)
        quantise_x(0, 0, 2)
        flip_w(0, 0, 1, vec, next_bank())
        flip_w(0, 0, 2, act, next_bank())
        keep_clock(1)
        for g in range(PASSES):
            quantise_w(0, 0, g)
        flip_x(0, 1, 0, act)
        keep_clock(1)
        flip_x(0, 1, 1, vec)
        flip_x(0, 1, 2, act)
        bias_tile = next_bank()
        bias_bank = bias_tile[:].rearrange("p a u r -> p (a u r)")
        nc.tensor.transpose(bias_bank[:, 0:P], bias_rows[:].bitcast(F32), ident[:])
        bias_all = const.tile([P, 4 * n_rows], F32)
        nc.vector.tensor_copy(out=bias_all[:], in_=bias_bank.bitcast(BF16)[:, 0 : 4 * n_rows])
        bias_in = bias_all[:, 0 : 2 * n_rows]
        bias_hid = bias_all[:, 2 * n_rows : 4 * n_rows]
        bias_both = const.tile([P, 2 * n_rows], F32)
        nc.gpsimd.tensor_tensor(out=bias_both[:], in0=bias_in, in1=bias_hid, op=ALU.add)
        bias_both_negative = const.tile([P, 2 * n_rows], F32)
        nc.gpsimd.tensor_scalar(out=bias_both_negative[:], in0=bias_both[:], scalar1=-1.0, scalar2=None, op0=ALU.mult)

        for unit in first_units:
            reset_gate(unit, HALVES[0])
        for g in range(PASSES):
            quantise_x(0, 1, g)
        flip_w(0, 1, 0, act, next_bank())
        flip_w(0, 1, 1, vec, next_bank())
        flip_w(0, 1, 2, act, next_bank())
        for unit in first_units:
            reset_gate(unit, HALVES[1])
        for g in range(PASSES):
            quantise_w(0, 1, g)
        for g in range(PASSES):
            flip_w(0, 2, g, shares[g], next_bank())
        for g in range(PASSES):
            quantise_w(0, 2, g)
        for unit in first_units:
            update_gate(unit)
        for g in range(PASSES):
            flip_x(1, 0, g, act)
        for g in range(PASSES):
            quantise_x(1, 0, g)
        for unit in first_units:
            hidden_sums(unit)
            gate_hidden(unit)
        for g in range(PASSES):
            flip_x(1, 1, g, act)
        for unit in first_units:
            input_sums(unit)
        for g in range(PASSES):
            quantise_x(1, 1, g)
        for unit in first_units:
            candidate_input(unit)
        for g in range(PASSES):
            flip_w(1, 0, g, act, next_bank())
        for unit in first_units:
            candidate(unit)
        difference(first_units[0], nc.gpsimd)
        load_w(2, 0)
        for g in range(PASSES):
            quantise_w(1, 0, g)
        change(first_units[0], nc.vector)
        previous = first_units[1]

        weight_banks_taken = [0]

        def weight_bank():
            bank = flipped.tile([P, 2, 2, P], F32, tag="bank" + str(weight_banks_taken[0] % 3))
            weight_banks_taken[0] += 1
            return bank

        in_order = [(0, 0), (0, 1), (0, 2), (1, 0), (1, 1), (1, 2), (2, 1), (2, 2), (2, 0)]
        weight_rounds = {2: in_order[3:6], 3: in_order[6:9]}
        for pair in range(1, PAIRS - 1):
            first_round = pair * 2 * CHUNKS
            weight_rounds[first_round] = in_order[0:3]
            for step in range(1, 2 * CHUNKS):
                weight_rounds[first_round + step] = in_order[2 * step + 1 : 2 * step + 3]


        return_rounds = {}
        for rnd in range(RETURN_LAG, ROUNDS - 2 * CHUNKS):
            return_rounds[rnd] = [rnd - RETURN_LAG]
        return_rounds[13] = [9, 10, 11]
        waiting = []
        for rnd in range(2, ROUNDS - 1):
            pair, step = divmod(rnd, 2 * CHUNKS)
            chunk, e = divmod(step, 2)
            next_banks = weight_rounds.get(rnd, [])
            last_pair = pair == PAIRS - 1

            unit = {"where": (pair, chunk, e)}
            reset_gate(unit)
            update_gate(unit)
            hidden_sums(unit)
            input_sums(unit)
            difference(previous, nc.gpsimd)
            for bank_number, bank in waiting:
                add_state_and_store(bank_number, bank)
            if last_pair:
                change(previous, nc.gpsimd)
            gate_hidden(unit)
            candidate_input(unit)
            for gate, g in next_banks:
                flip_w(pair + 1, gate, g, act, weight_bank())
            if rnd < ROUNDS - 2:
                candidate(unit)
            waiting = []
            for bank_number in return_rounds.get(rnd, []):
                waiting.append((bank_number, flip_results(bank_number, bank_number % 4 if last_pair else 3)))
            if pair + 2 < PAIRS and step > 0:
                load_w(pair + 2, step - 1)
            for gate, g in next_banks:
                quantise_w(pair + 1, gate, g)
            if not last_pair:
                change(previous, nc.vector)
            previous = unit


        last_away = apart.tile([P, CHUNK], F32)
        unit = {"where": (PAIRS - 1, CHUNKS - 1, 1), "away": last_away}
        left, right = HALVES
        reset_gate(unit, left)
        candidate(previous)
        hidden_sums(unit, left)
        input_sums(unit, left)
        spare = flipped.tile([P, CHUNK], F32, tag="bank2")
        update_gate(unit, left, spare)
        for bank_number, bank in waiting:
            add_state_and_store(bank_number, bank)
        gate_hidden(unit, left)
        reset_gate(unit, right)
        candidate_input(unit, left)
        candidate(unit, left)
        difference(previous, nc.vector)
        hidden_sums(unit, right)
        input_sums(unit, right)
        update_gate(unit, right)
        gate_hidden(unit, right)
        difference(unit, nc.vector, left)
        candidate_input(unit, right)
        candidate(unit, right)
        bank_even = return_with_state(ROUNDS - 4, 0)
        copy_and_store(ROUNDS - 4, bank_even)
        bank_odd = flip_results(ROUNDS - 3, 1)
        change(previous, nc.vector)
        change(unit, nc.vector, left)
        bank_left = flip_results(ROUNDS - 2, 2)
        difference(unit, nc.vector, right)
        add_state_and_store(ROUNDS - 3, bank_odd)
        change(unit, nc.vector, right)
        add_state_and_store(ROUNDS - 2, bank_left)
        bank_right = flip_results(ROUNDS - 1, 3)
        add_state_and_store(ROUNDS - 1, bank_right, (0, 1))
        add_state_and_store(ROUNDS - 1, bank_right, (1, 2))
